import numpy as np
import ml_dtypes


def mxq(x, axis, fmt="e4m3"):
    dtype, down = {"e4m3": (ml_dtypes.float8_e4m3fn, 7), "e5m2": (ml_dtypes.float8_e5m2, 14)}[fmt]
    v = np.moveaxis(np.asarray(x, np.float32).astype(ml_dtypes.bfloat16).astype(np.float64), axis, -1)
    blocks = v.reshape(v.shape[:-1] + (-1, 32))
    amax = np.abs(blocks).max(-1, keepdims=True)
    byte = np.maximum(np.where(amax > 0, np.frexp(amax)[1] - 1 + 127, 0) - down, 1)
    scale = np.exp2(byte - 127.0)
    codes = (blocks / scale).astype(np.float32).astype(dtype).astype(np.float64)
    return np.moveaxis((codes * scale).reshape(v.shape), -1, axis)


WIDE = False


def mx_kscale(k):
    if not WIDE:
        return np.ones(k)
    levels = np.array([18, -18])
    if k % 512:
        return np.exp2(np.random.permutation(np.resize(levels, k // 32))).repeat(32)
    a = np.empty((k // 512, 16))
    for p in range(k // 512):
        a[p, :8] = np.random.permutation(np.resize(levels, 8))
        for g in range(8):
            far = levels[np.abs(levels - a[p, g]) >= 10]
            a[p, g + 8] = far[np.random.randint(len(far))]
    return np.exp2(a.ravel()).repeat(32)


BF16 = ml_dtypes.bfloat16


def bf(x):
    return np.asarray(x, np.float32).astype(BF16)


def f64(x):
    return np.asarray(x).astype(np.float64)


B, K, NH, N = 1024, 2048, 512, 1024
EPSILON = 0.1


def setup_inputs():
    s = mx_kscale(B)[:, None]
    u = mx_kscale(N)
    x0 = bf(np.random.standard_normal((B, K)))
    y0 = bf(np.random.standard_normal((B, N)) * 4.0)
    sgn = np.where(np.random.random((K, N)) < 0.5, -1.0, 1.0)
    beta0 = bf(sgn * (0.1 + 0.9 * np.random.random((K, N))) * 1.7 / np.sqrt(K))
    bias_lin = bf(np.random.standard_normal(N) * 0.1)
    W1 = bf(-np.random.random((NH, K)) * 1.7 / np.sqrt(K))
    W2 = bf(np.random.random((N, NH)) * (0.5 + np.random.random((N, 1))) * 2.0 / NH**2)
    bias1 = bf(np.random.standard_normal(NH) * 0.1)
    bias2 = bf(np.random.standard_normal(N) * 0.1)
    g = bf(4.0 * np.random.standard_normal((B, N)) * np.exp2(np.random.randint(-6, 1, (B, 1))) / s * u)
    return {"x": bf(f64(x0) * s),
            "y": bf(f64(y0) * s),
            "beta": bf(f64(beta0) / u),
            "bias_lin": bias_lin,
            "W1": W1,
            "W2": W2,
            "bias1": bias1,
            "bias2": bias2,
            "adv": 1,
            "grad_out": g}


def reference(x, y, beta, bias_lin, W1, W2, bias1, bias2, adv, grad_out):
    g = f64(grad_out)
    bt = f64(beta)
    dx = mxq(g, 1, "e5m2") @ mxq(bt, 1, "e4m3").T
    dbeta = mxq(f64(x), 0, "e4m3").T @ mxq(g, 0, "e5m2")
    if adv:
        r = np.sum(g * f64(y), axis=0)
        dbeta = dbeta - EPSILON * np.sign(bt) * r
    return dx, dbeta

@@ -1,0 +1,318 @@
+from contextlib import ExitStack
+
+import concourse.mybir as mybir
+from concourse.masks import make_identity
+
+B, K, N = 1024, 2048, 1024
+EPSILON = 0.1
+FLOPS = 2 * 2 * B * K * N
+BYTES = 2 * (B * K + 2 * B * N + K * N) + 4 * (B * K + K * N)
+
+F32 = mybir.dt.float32
+BF16 = mybir.dt.bfloat16
+U32 = mybir.dt.uint32
+U8 = mybir.dt.uint8
+E4M3 = mybir.dt.float8_e4m3fn_x4
+E5M2 = mybir.dt.float8_e5m2_x4
+ALU = mybir.AluOpType
+
+P = 128
+PACK = 4
+PASS = P * PACK
+BANK = 512
+WIDE = 1024
+LIFT = 2.0**100
+STEP = 2.0**-33
+GROUPED_BUFS = 4
+XI_BUFS = 4
+X_AHEAD = 3
+AHEAD = 4
+LIFT_BUFS = 3
+WIDE_BUFS = 3
+DB_BUFS = 8
+WARM = 11
+FAST = 8
+TURN_ODD = 0
+
+
+def tile_advresnet_v_kernel(
+    tc, x, y, beta, bias_lin, W1, W2, bias1, bias2, adv, grad_out, out_0, out_1
+):
+    nc = tc.nc
+    assert adv == 1
+    with ExitStack() as ctx:
+        keep = ctx.enter_context(tc.tile_pool(name="keep", bufs=1))
+        work = ctx.enter_context(tc.tile_pool(name="work", bufs=GROUPED_BUFS))
+        stage = ctx.enter_context(tc.tile_pool(name="stage", bufs=1))
+        psum = ctx.enter_context(tc.psum_pool(name="psum", bufs=4))
+        ctx.enter_context(tc.manual_schedule())
+
+        def load(name, src, pool=keep, tag="", bufs=1):
+            t = pool.tile([P, PACK, src.shape[2]], BF16, name=name, tag=tag, bufs=bufs, align_bytes=64)
+            nc.sync.dma_start(out=t[:], in_=src)
+            return t
+
+        def token_rows(src, grp, c0, width=WIDE):
+            return src[grp * PASS : (grp + 1) * PASS, c0 : c0 + width].rearrange("(p j) w -> p j w", j=PACK)
+
+        def beta_rows(kc):
+            return beta[kc * BANK : (kc + 1) * BANK, :].rearrange("(t p) n -> p t n", p=P)
+
+        def new_bank(name, reader):
+            bank = psum.tile([P, BANK], F32, name=name, tag=reader)
+            return bank
+
+        def new_grouped(name):
+            grouped = work.tile([P, BANK * PACK], BF16, name=name, tag="grouped", align_bytes=64)
+            return grouped
+
+        def interleave(copy, dst, src):
+            copy(
+                out=dst.rearrange("p (c i t) -> p c t i", i=4, t=PACK),
+                in_=src.rearrange("p t (c i) -> p c t i", i=4),
+            )
+
+        def transpose_pair(name, raw, grp, pair):
+            bank = new_bank(name, "scalar")
+            words = raw[:].bitcast(F32)
+            w0 = grp * PASS // 2
+            for a in range(2):
+                for u in range(2):
+                    c0 = (2 * a + u) * P
+                    nc.tensor.transpose(
+                        bank[:, c0 : c0 + P], words[:, 2 * pair + a, w0 + u : w0 + PASS // 2 : 2], ident[:]
+                    )
+            return bank
+
+        def empty_pair(grouped, bank, pair):
+            words = grouped[:].bitcast(F32)[:, pair * BANK : (pair + 1) * BANK]
+            nc.scalar.copy(
+                out=words.rearrange("p (a r u) -> p a r u", a=2, u=2),
+                in_=bank[:].rearrange("p (a u r) -> p a r u", a=2, u=2),
+            )
+
+        def transposed(name, raw, grp):
+            banks = [transpose_pair("%s_ps%d" % (name, pair), raw, grp, pair) for pair in range(2)]
+            grouped = new_grouped(name)
+            for pair in range(2):
+                empty_pair(grouped, banks[pair], pair)
+            return grouped
+
+        def quantize(name, grouped, fmt):
+            width = grouped.shape[1] // PACK
+            codes = keep.tile([P, width], U32, name=name + "_codes", align_bytes=64)
+            scales = keep.tile([P, width], U8, name=name + "_scales", align_bytes=64)
+            nc.vector.quantize_mx(out=codes[:].bitcast(fmt), scales=scales[:], in_=grouped[:])
+            return codes, scales, fmt
+
+        def product(name, reader, stationary, m, moving):
+            bank = new_bank(name, reader)
+            cols = slice(m * P, (m + 1) * P)
+            for grp in range(2):
+                lc, ls, lf = stationary[grp]
+                rc, rs, rf = moving[grp]
+                nc.tensor.matmul_mx(
+                    out=bank[:],
+                    lhsT=lc[:, cols].bitcast(lf),
+                    lhsT_scale=ls[:, cols],
+                    rhs=rc[:].bitcast(rf),
+                    rhs_scale=rs[:],
+                    start=(grp == 0),
+                    stop=(grp == 1),
+                )
+            return bank
+
+        dx_rows = {}
+
+        def dx_group(index):
+            half, rest = divmod(index, 16)
+            rest, side = divmod(rest, 2)
+            kc = 2 * half + side
+            grp, j = divmod(rest, PACK)
+            pair, a = divmod(j, 2)
+            if side == 0 and a == 0:
+                dx_rows[grp, pair] = stage.tile([P, 2, WIDE], F32, name="dx%d%d%d" % (grp, pair, half), tag="wide", bufs=WIDE_BUFS, align_bytes=64)
+            rows = dx_rows[grp, pair]
+            bank = product("dx_ps%d%d%d" % (grp, j, kc), "scalar", g_feat[grp], j, b_feat[kc])
+            nc.scalar.copy(out=rows[:, a, side * BANK : (side + 1) * BANK], in_=bank[:])
+            if side == 1:
+                dst = out_0[grp * PASS : (grp + 1) * PASS, half * WIDE : (half + 1) * WIDE]
+                nc.sync.dma_start(out=dst.rearrange("(p j) k -> p j k", j=PACK)[:, j, :], in_=rows[:, a, :])
+
+        def gy_part(bank, nh, grp):
+            for q in range(4):
+                cols = slice(nh * BANK + q * P, nh * BANK + (q + 1) * P)
+                for j in range(PACK):
+                    nc.tensor.matmul(
+                        out=bank[:, q * P : (q + 1) * P],
+                        lhsT=g_raw[grp][:, j, cols],
+                        rhs=y_raw[grp][:, j, cols],
+                        start=(grp == 0 and q == 0 and j == 0),
+                        stop=(grp == 1 and q == 3 and j == PACK - 1),
+                    )
+
+        def mask_half(nh, bank):
+            nc.vector.scalar_tensor_tensor(
+                out=diag[:, nh * BANK : (nh + 1) * BANK].rearrange("p (q c) -> p q c", q=4),
+                in0=bank[:].rearrange("p (q c) -> p q c", q=4),
+                scalar=-EPSILON,
+                in1=ident[:].unsqueeze(1).to_broadcast([P, 4, P]),
+                op0=ALU.mult,
+                op1=ALU.mult,
+            )
+
+        def spread_half(nh):
+            bank = new_bank("shift%d" % nh, "scalar")
+            cols = slice(nh * BANK, (nh + 1) * BANK)
+            nc.tensor.matmul(out=bank[:], lhsT=big[:], rhs=diag[:, cols], start=True, stop=True)
+            nc.scalar.copy(out=shift[:, cols], in_=bank[:])
+
+        lifted = {}
+
+        def lift(kt):
+            kc, t = divmod(kt, 4)
+            lifted[kt] = work.tile([P, WIDE], BF16, name="lifted%d" % kt, tag="lifted", bufs=LIFT_BUFS)
+            nc.vector.tensor_scalar(
+                out=lifted[kt][:], in0=b_raw[kc][:, t, :], scalar1=LIFT, scalar2=-STEP, op0=ALU.mult, op1=ALU.max
+            )
+
+        db_rows = {}
+
+        def db_shift(kt):
+            db_rows[kt] = stage.tile([P, WIDE], F32, name="db%d" % kt, tag="db", bufs=DB_BUFS)
+            nc.vector.scalar_tensor_tensor(
+                out=db_rows[kt][:], in0=lifted[kt][:], scalar=STEP, in1=shift[:], op0=ALU.min, op1=ALU.mult
+            )
+
+        def db_product(kt, nh):
+            codes, scales, fmt = x_tok[kt]
+            halves = [(codes[:, grp * P : (grp + 1) * P], scales[:, grp * P : (grp + 1) * P], fmt) for grp in range(2)]
+            return product("db_ps%d_%d" % (kt, nh), "vector", halves, 0, g_tok[nh])
+
+        def db_add(kt, nh, bank):
+            cols = slice(nh * BANK, (nh + 1) * BANK)
+            nc.vector.tensor_tensor(out=db_rows[kt][:, cols], in0=bank[:], in1=db_rows[kt][:, cols], op=ALU.add)
+            if nh == 1:
+                nc.sync.dma_start(out=out_1[kt * P : (kt + 1) * P, :], in_=db_rows[kt][:])
+
+        ident = keep.tile([P, P], F32, name="ident")
+        big = keep.tile([P, P], F32, name="big")
+        diag = keep.tile([P, N], F32, name="diag")
+        shift = keep.tile([P, N], F32, name="shift")
+
+        g_raw, y_raw, b_raw, x_raw = [], [], {}, {}
+        for grp in range(2):
+            g_raw.append(load("g%d" % grp, token_rows(grad_out, grp, 0)))
+            y_raw.append(load("y%d" % grp, token_rows(y, grp, 0), stage, "wide", WIDE_BUFS))
+        b_raw[0] = load("b0", beta_rows(0))
+        for kc in range(2):
+            for grp in range(2):
+                x_raw[kc, grp] = load("x%d%d" % (kc, grp), token_rows(x, grp, kc * BANK, BANK))
+            b_raw[kc + 1] = load("b%d" % (kc + 1), beta_rows(kc + 1))
+        b_raw[3] = load("b3", beta_rows(3))
+        for grp in range(2):
+            x_raw[2, grp] = load("x2%d" % grp, token_rows(x, grp, WIDE))
+        make_identity(nc, ident[:])
+        nc.vector.memset(big[:], 1.0 / STEP)
+
+        g_tok = [[None, None], [None, None]]
+        g_feat = [[None, None], [None, None]]
+        b_feat = [[None, None] for kc in range(4)]
+        x_tok = {}
+        x_grouped = {}
+
+        def g_tokens(grp):
+            inter = []
+            for nh in range(2):
+                inter.append(new_grouped("gi%d%d" % (grp, nh)))
+                interleave(nc.vector.tensor_copy, inter[nh][:], g_raw[grp][:, :, nh * BANK : (nh + 1) * BANK])
+            return inter
+
+        def g_tok_quant(grp, nh, grouped):
+            g_tok[nh][grp] = quantize("gtok%d%d" % (nh, grp), grouped, E5M2)
+
+        def g_turn(grp, nh):
+            return transposed("gt%d%d" % (grp, nh), g_raw[grp], nh)
+
+        def g_quant(grp, nh, turned):
+            g_feat[grp][nh] = quantize("gfeat%d%d" % (grp, nh), turned, E5M2)
+
+        def b_turn(kc, nh):
+            return transposed("bt%d%d" % (kc, nh), b_raw[kc], nh)
+
+        def b_quant(kc, nh, turned):
+            b_feat[kc][nh] = quantize("bfeat%d%d" % (kc, nh), turned, E4M3)
+
+        def x_inter(kt, grp, copy=nc.scalar.copy):
+            if grp == 0:
+                x_grouped[kt] = work.tile([P, 2 * BANK], BF16, name="xi%d" % kt, tag="xi", bufs=XI_BUFS, align_bytes=64)
+            part = min(kt // 4, 2)
+            t = kt - 4 * part
+            interleave(copy, x_grouped[kt][:, grp * BANK : (grp + 1) * BANK], x_raw[part, grp][:, :, t * P : (t + 1) * P])
+
+        def x_quant(kt):
+            x_tok[kt] = quantize("xtok%d" % kt, x_grouped[kt], E4M3)
+
+        zeros = keep.tile([P, BANK], BF16, name="zeros")
+        nc.vector.memset(zeros[:], 0.0)
+        warm = new_bank("warm", "vector")
+        for s in range(WARM):
+            nc.tensor.matmul(out=warm[:], lhsT=zeros[:, :P], rhs=zeros[:], start=True, stop=True)
+
+        gy = [new_bank("gy%d" % nh, "vector") for nh in range(2)]
+        inter = g_tokens(0)
+        turned = [g_turn(0, nh) for nh in range(2)]
+        for nh in range(2):
+            g_tok_quant(0, nh, inter[nh])
+        for nh in range(2):
+            gy_part(gy[nh], nh, 0)
+            g_quant(0, nh, turned[nh])
+        inter = g_tokens(1)
+        turned = [g_turn(1, nh) for nh in range(2)]
+        for nh in range(2):
+            gy_part(gy[nh], nh, 1)
+        for nh in range(2):
+            g_quant(1, nh, turned[nh])
+            mask_half(nh, gy[nh])
+            spread_half(nh)
+            x_inter(0, nh)
+        for nh in range(2):
+            g_tok_quant(1, nh, inter[nh])
+        lift(0)
+        for unit in range(4):
+            kc, nh = divmod(unit, 2)
+            turned = b_turn(kc, nh)
+            if unit < 2 * (X_AHEAD - 1):
+                x_inter(1 + kc, nh)
+            lift(unit + 1)
+            if unit < AHEAD:
+                db_shift(unit)
+            b_quant(kc, nh, turned)
+            if nh == 0 and kc < X_AHEAD - 1:
+                x_quant(kc)
+
+        turned = {}
+        index = 0
+        for kt in range(16):
+            turning = kt % 2 == TURN_ODD and kt < 8
+            banks = []
+            for nh in range(2):
+                banks.append(db_product(kt, nh))
+                if nh == 1 and turning:
+                    turned[kt] = b_turn(2 + kt // 4, kt // 2 % 2)
+                for s in range(2 if nh == 1 and not turning and kt >= FAST else 1):
+                    if index < 32:
+                        dx_group(index)
+                        index = index + 1
+                if kt + X_AHEAD < 16:
+                    x_inter(kt + X_AHEAD, nh)
+            if kt + AHEAD < 16:
+                db_shift(kt + AHEAD)
+            if kt + X_AHEAD - 1 < 16:
+                x_quant(kt + X_AHEAD - 1)
+            db_add(kt, 0, banks[0])
+            if kt + 5 < 16:
+                lift(kt + 5)
+            if kt - 1 in turned:
+                b_quant(2 + (kt - 1) // 4, (kt - 1) // 2 % 2, turned[kt - 1])
+            db_add(kt, 1, banks[1])

@@ -15,6 +15,7 @@ U8 = mybir.dt.uint8
 E4M3 = mybir.dt.float8_e4m3fn_x4
 E5M2 = mybir.dt.float8_e5m2_x4
 ALU = mybir.AluOpType
+ACT = mybir.ActivationFunctionType
 
 P = 128
 PACK = 4
@@ -23,16 +24,47 @@ BANK = 512
 WIDE = 1024
 LIFT = 2.0**100
 STEP = 2.0**-33
-GROUPED_BUFS = 4
-XI_BUFS = 4
-X_AHEAD = 3
-AHEAD = 4
-LIFT_BUFS = 3
-WIDE_BUFS = 3
-DB_BUFS = 8
-WARM = 11
-FAST = 8
-TURN_ODD = 0
+GROUPED_BUFS = 3
+XI_BUFS = 2
+X_AHEAD = 2
+AHEAD = 2
+WIDE_BUFS = 8
+WARM = 12
+POOL_FROM = 1
+XI_AT = 4
+LEAD = 6
+X_CUTS = [0, 1024, 2048]
+LOADS = [("b", 0), ("b", 1), ("x", 0), ("b", 2), ("b", 3), ("x", 1)]
+DX_RATE = [3, 3, 3, 3, 4, 5, 5, 5]
+DB_LEAD = 2
+ORDER = [0, 2, 1, 3]
+TURN_AT = [-2, -1, 2, 4, 6, 8]
+TURN_LAG = 3
+DX_NUM = 9
+DX_DEN = 8
+X_LEAD = 8
+BT1_AT = [0, 1]
+XQ_AT = 2
+SHIFT_LEAD = 4
+LIFT_LEAD = 3
+FIRST = [4, 0]
+G11_FIRST = False
+BANKS = {"vector": 3, "scalar": 3, "shift": 2}
+SIGN_PAIRS = [3, 4, 5, 6, 7]
+SIGN_AT = [0, 1]
+LIFT_BUFS = 4
+QUANT_AT = [2]
+XP_BUFS = 1
+STORE_LAG = 2
+GI_VECTOR = 2
+FILL_NUM = 3
+FILL_DEN = 2
+DX_PER_TURN = 1
+SINCE = 0
+X01_VECTOR = True
+X_FIRST = False
+WHOLE = []
+SIGN_LEAD = 14
 
 
 def tile_advresnet_v_kernel(
@@ -42,74 +74,72 @@ def tile_advresnet_v_kernel(
     assert adv == 1
     with ExitStack() as ctx:
         keep = ctx.enter_context(tc.tile_pool(name="keep", bufs=1))
-        work = ctx.enter_context(tc.tile_pool(name="work", bufs=GROUPED_BUFS))
-        stage = ctx.enter_context(tc.tile_pool(name="stage", bufs=1))
-        psum = ctx.enter_context(tc.psum_pool(name="psum", bufs=4))
+        work = ctx.enter_context(tc.tile_pool(name="work", bufs=1))
+        wide = ctx.enter_context(tc.tile_pool(name="wide", bufs=WIDE_BUFS))
+        psum = ctx.enter_context(tc.psum_pool(name="psum", bufs=1))
         ctx.enter_context(tc.manual_schedule())
 
-        def load(name, src, pool=keep, tag="", bufs=1):
-            t = pool.tile([P, PACK, src.shape[2]], BF16, name=name, tag=tag, bufs=bufs, align_bytes=64)
-            nc.sync.dma_start(out=t[:], in_=src)
-            return t
-
-        def token_rows(src, grp, c0, width=WIDE):
+        def token_rows(src, grp, c0, width):
             return src[grp * PASS : (grp + 1) * PASS, c0 : c0 + width].rearrange("(p j) w -> p j w", j=PACK)
 
-        def beta_rows(kc):
-            return beta[kc * BANK : (kc + 1) * BANK, :].rearrange("(t p) n -> p t n", p=P)
+        g_raw, y_raw, b_raw, x_raw = {}, {}, {}, {}
+
+        def load_tokens(store, name, src, grp):
+            store[grp] = wide.tile([P, PACK, N], BF16, name="%s%d" % (name, grp), tag="wide", align_bytes=64)
+            nc.sync.dma_start(out=store[grp][:], in_=token_rows(src, grp, 0, N))
+
+        def load_beta(kc):
+            b_raw[kc] = keep.tile([P, PACK, N], BF16, name="b%d" % kc, align_bytes=64)
+            nc.sync.dma_start(
+                out=b_raw[kc][:].rearrange("p (d j) n -> p d (j n)", j=2),
+                in_=beta[kc * BANK : (kc + 1) * BANK, :].rearrange("(d p j) n -> p d (j n)", p=P, j=2),
+            )
+
+        def load_x(part, grp):
+            c0, c1 = X_CUTS[part], X_CUTS[part + 1]
+            x_raw[part, grp] = keep.tile([P, PACK, c1 - c0], BF16, name="x%d%d" % (part, grp))
+            nc.sync.dma_start(out=x_raw[part, grp][:], in_=token_rows(x, grp, c0, c1 - c0))
 
         def new_bank(name, reader):
-            bank = psum.tile([P, BANK], F32, name=name, tag=reader)
+            bank = psum.tile([P, BANK], F32, name=name, tag=reader, bufs=BANKS[reader])
             return bank
 
         def new_grouped(name):
-            grouped = work.tile([P, BANK * PACK], BF16, name=name, tag="grouped", align_bytes=64)
+            grouped = work.tile([P, BANK * PACK], BF16, name=name, tag="grouped", bufs=GROUPED_BUFS, align_bytes=64)
             return grouped
 
-        def interleave(copy, dst, src):
-            copy(
-                out=dst.rearrange("p (c i t) -> p c t i", i=4, t=PACK),
-                in_=src.rearrange("p t (c i) -> p c t i", i=4),
-            )
-
-        def transpose_pair(name, raw, grp, pair):
-            bank = new_bank(name, "scalar")
+        def transposed(name, raw, grp):
             words = raw[:].bitcast(F32)
             w0 = grp * PASS // 2
-            for a in range(2):
-                for u in range(2):
-                    c0 = (2 * a + u) * P
-                    nc.tensor.transpose(
-                        bank[:, c0 : c0 + P], words[:, 2 * pair + a, w0 + u : w0 + PASS // 2 : 2], ident[:]
-                    )
-            return bank
-
-        def empty_pair(grouped, bank, pair):
-            words = grouped[:].bitcast(F32)[:, pair * BANK : (pair + 1) * BANK]
-            nc.scalar.copy(
-                out=words.rearrange("p (a r u) -> p a r u", a=2, u=2),
-                in_=bank[:].rearrange("p (a u r) -> p a r u", a=2, u=2),
-            )
-
-        def transposed(name, raw, grp):
-            banks = [transpose_pair("%s_ps%d" % (name, pair), raw, grp, pair) for pair in range(2)]
+            banks = []
+            for pair in range(2):
+                banks.append(new_bank("%s_ps%d" % (name, pair), "scalar"))
+                for a in range(2):
+                    for u in range(2):
+                        c0 = (2 * a + u) * P
+                        nc.tensor.transpose(
+                            banks[pair][:, c0 : c0 + P], words[:, 2 * pair + a, w0 + u : w0 + PASS // 2 : 2], ident[:]
+                        )
             grouped = new_grouped(name)
             for pair in range(2):
-                empty_pair(grouped, banks[pair], pair)
+                dst = grouped[:].bitcast(F32)[:, pair * BANK : (pair + 1) * BANK]
+                nc.scalar.copy(
+                    out=dst.rearrange("p (a r u) -> p a r u", a=2, u=2),
+                    in_=banks[pair][:].rearrange("p (a u r) -> p a r u", a=2, u=2),
+                )
             return grouped
 
         def quantize(name, grouped, fmt):
-            width = grouped.shape[1] // PACK
-            codes = keep.tile([P, width], U32, name=name + "_codes", align_bytes=64)
-            scales = keep.tile([P, width], U8, name=name + "_scales", align_bytes=64)
+            codes = keep.tile([P, BANK], U32, name=name + "_codes", align_bytes=64)
+            scales = keep.tile([P, BANK], U8, name=name + "_scales", align_bytes=64)
             nc.vector.quantize_mx(out=codes[:].bitcast(fmt), scales=scales[:], in_=grouped[:])
             return codes, scales, fmt
 
-        def product(name, reader, stationary, m, moving):
+        def product(name, reader, stationary, moving):
             bank = new_bank(name, reader)
-            cols = slice(m * P, (m + 1) * P)
             for grp in range(2):
-                lc, ls, lf = stationary[grp]
+                (lc, ls, lf), m = stationary[grp]
+                cols = slice(m * P, (m + 1) * P)
                 rc, rs, rf = moving[grp]
                 nc.tensor.matmul_mx(
                     out=bank[:],
@@ -122,25 +152,88 @@ def tile_advresnet_v_kernel(
                 )
             return bank
 
-        dx_rows = {}
+        g_tok = [[None, None], [None, None]]
+        g_feat = [[None, None], [None, None]]
+        b_feat = [[None, None] for kc in range(4)]
+        x_tok, x_grouped, dx_rows, db_rows, lifted = {}, {}, {}, {}, {}
+
+        def g_inter(grp, nh, copy):
+            grouped = work.tile([P, BANK * PACK], BF16, name="gi%d%d" % (grp, nh), tag="xi", bufs=XI_BUFS, align_bytes=64)
+            copy(
+                out=grouped[:].rearrange("p (c i t) -> p c t i", i=4, t=PACK),
+                in_=g_raw[grp][:, :, nh * BANK : (nh + 1) * BANK].rearrange("p t (c i) -> p c t i", i=4),
+            )
+            return grouped
+
+        def g_tok_quant(grp, nh, grouped):
+            g_tok[nh][grp] = quantize("gtok%d%d" % (nh, grp), grouped, E5M2)
+
+        def g_turn(grp, nh):
+            return transposed("gt%d%d" % (grp, nh), g_raw[grp], nh)
+
+        def g_quant(grp, nh, turned):
+            g_feat[grp][nh] = quantize("gfeat%d%d" % (grp, nh), turned, E5M2)
+
+        def b_turn(kc, nh):
+            return transposed("bt%d%d" % (kc, nh), b_raw[kc], nh)
+
+        def b_quant(kc, nh, turned):
+            b_feat[kc][nh] = quantize("bfeat%d%d" % (kc, nh), turned, E4M3)
+
+        def x_inter(d, grp, copy=nc.scalar.copy):
+            on_pool = d >= POOL_FROM
+            if grp == 0:
+                tag, bufs = ("xp", XP_BUFS)
+                x_grouped[d] = work.tile([P, BANK * PACK], BF16, name="xi%d" % d, tag=tag, bufs=bufs, align_bytes=64)
+            part = max(s for s in range(len(X_CUTS) - 1) if X_CUTS[s] <= 2 * P * d)
+            c0 = 2 * P * d - X_CUTS[part]
+            dst = x_grouped[d][:, grp * 2 * BANK : (grp + 1) * 2 * BANK]
+            src = x_raw[part, grp][:, :, c0 : c0 + 2 * P]
+            if on_pool:
+                nc.gpsimd.tensor_scalar(
+                    out=dst.rearrange("p (j m t) -> p j m t", j=2, t=PACK),
+                    in0=src.rearrange("p t (m j) -> p j m t", j=2),
+                    scalar1=1.0,
+                    scalar2=0.0,
+                    op0=ALU.mult,
+                    op1=ALU.add,
+                )
+            else:
+                copy(
+                    out=dst.rearrange("p (j c m t) -> p c t m j", j=2, m=2, t=PACK),
+                    in_=src.rearrange("p t (c m j) -> p c t m j", m=2, j=2),
+                )
+
+        def x_quant(d):
+            x_tok[d] = quantize("xtok%d" % d, x_grouped[d], E4M3)
+
+        dx_done = []
 
         def dx_group(index):
             half, rest = divmod(index, 16)
-            rest, side = divmod(rest, 2)
-            kc = 2 * half + side
+            if rest < 2 * FIRST[half]:
+                side, rest = divmod(rest, FIRST[half])
+            else:
+                rest, side = divmod(rest, 2)
             grp, j = divmod(rest, PACK)
             pair, a = divmod(j, 2)
+            kc = 2 * half + side
             if side == 0 and a == 0:
-                dx_rows[grp, pair] = stage.tile([P, 2, WIDE], F32, name="dx%d%d%d" % (grp, pair, half), tag="wide", bufs=WIDE_BUFS, align_bytes=64)
+                dx_rows[grp, pair] = wide.tile(
+                    [P, 2, WIDE], F32, name="dx%d%d%d" % (grp, pair, half), tag="wide", align_bytes=64
+                )
             rows = dx_rows[grp, pair]
-            bank = product("dx_ps%d%d%d" % (grp, j, kc), "scalar", g_feat[grp], j, b_feat[kc])
-            nc.scalar.copy(out=rows[:, a, side * BANK : (side + 1) * BANK], in_=bank[:])
+            bank = product("dx_ps%d%d%d" % (grp, j, kc), "scalar", [(g_feat[grp][nh], j) for nh in range(2)], b_feat[kc])
+            nc.scalar.copy(
+                out=rows[:, a, side * BANK : (side + 1) * BANK].rearrange("p (d r j) -> p d r j", d=2, j=2),
+                in_=bank[:].rearrange("p (d j r) -> p d r j", d=2, j=2),
+            )
             if side == 1:
                 dst = out_0[grp * PASS : (grp + 1) * PASS, half * WIDE : (half + 1) * WIDE]
-                nc.sync.dma_start(out=dst.rearrange("(p j) k -> p j k", j=PACK)[:, j, :], in_=rows[:, a, :])
+                dx_done.append((dst.rearrange("(p j) k -> p j k", j=PACK)[:, j, :], rows[:, a, :]))
 
-        def gy_part(bank, nh, grp):
-            for q in range(4):
+        def gy_part(bank, nh, grp, blocks=range(4)):
+            for q in blocks:
                 cols = slice(nh * BANK + q * P, nh * BANK + (q + 1) * P)
                 for j in range(PACK):
                     nc.tensor.matmul(
@@ -162,157 +255,174 @@ def tile_advresnet_v_kernel(
             )
 
         def spread_half(nh):
-            bank = new_bank("shift%d" % nh, "scalar")
+            shift[nh] = new_bank("shift%d" % nh, "shift")
+            nc.tensor.matmul(out=shift[nh][:], lhsT=big[:], rhs=diag[:, nh * BANK : (nh + 1) * BANK], start=True, stop=True)
+
+        def lift(d):
+            kc, side = divmod(d, 2)
+            lifted[d] = work.tile([P, 2, N], BF16, name="lifted%d" % d, tag="lifted", bufs=LIFT_BUFS)
+            dst = lifted[d][:].rearrange("p j n -> p (j n)")
+            src = b_raw[kc][:, 2 * side : 2 * side + 2, :].rearrange("p j n -> p (j n)")
+            if d not in SIGN_PAIRS:
+                nc.vector.tensor_scalar(out=dst, in0=src, scalar1=LIFT, scalar2=-STEP, op0=ALU.mult, op1=ALU.max)
+
+        def sign(d, q):
+            kc, side = divmod(d, 2)
+            j, nh = divmod(q, 2)
+            if q == 0:
+                lifted[d] = work.tile([P, 2, N], BF16, name="lifted%d" % d, tag="lifted", bufs=LIFT_BUFS)
             cols = slice(nh * BANK, (nh + 1) * BANK)
-            nc.tensor.matmul(out=bank[:], lhsT=big[:], rhs=diag[:, cols], start=True, stop=True)
-            nc.scalar.copy(out=shift[:, cols], in_=bank[:])
+            nc.scalar.activation(out=lifted[d][:, j, cols], in_=b_raw[kc][:, 2 * side + j, cols], func=ACT.Sign)
 
-        lifted = {}
-
-        def lift(kt):
-            kc, t = divmod(kt, 4)
-            lifted[kt] = work.tile([P, WIDE], BF16, name="lifted%d" % kt, tag="lifted", bufs=LIFT_BUFS)
-            nc.vector.tensor_scalar(
-                out=lifted[kt][:], in0=b_raw[kc][:, t, :], scalar1=LIFT, scalar2=-STEP, op0=ALU.mult, op1=ALU.max
-            )
-
-        db_rows = {}
-
-        def db_shift(kt):
-            db_rows[kt] = stage.tile([P, WIDE], F32, name="db%d" % kt, tag="db", bufs=DB_BUFS)
+        def db_shift(d, nh):
+            if nh == 0:
+                db_rows[d] = wide.tile([P, 2, N], F32, name="db%d" % d, tag="wide", align_bytes=64)
+            cols = slice(nh * BANK, (nh + 1) * BANK)
             nc.vector.scalar_tensor_tensor(
-                out=db_rows[kt][:], in0=lifted[kt][:], scalar=STEP, in1=shift[:], op0=ALU.min, op1=ALU.mult
+                out=db_rows[d][:, :, cols],
+                in0=lifted[d][:, :, cols],
+                scalar=STEP,
+                in1=shift[nh][:].unsqueeze(1).to_broadcast([P, 2, BANK]),
+                op0=ALU.mult if d in SIGN_PAIRS else ALU.min,
+                op1=ALU.mult,
             )
 
-        def db_product(kt, nh):
-            codes, scales, fmt = x_tok[kt]
-            halves = [(codes[:, grp * P : (grp + 1) * P], scales[:, grp * P : (grp + 1) * P], fmt) for grp in range(2)]
-            return product("db_ps%d_%d" % (kt, nh), "vector", halves, 0, g_tok[nh])
+        def db_product(d, j, nh):
+            return product("db_ps%d%d%d" % (d, j, nh), "vector", [(x_tok[d], 2 * grp + j) for grp in range(2)], g_tok[nh])
 
-        def db_add(kt, nh, bank):
+        def db_add(d, j, nh, bank):
             cols = slice(nh * BANK, (nh + 1) * BANK)
-            nc.vector.tensor_tensor(out=db_rows[kt][:, cols], in0=bank[:], in1=db_rows[kt][:, cols], op=ALU.add)
-            if nh == 1:
-                nc.sync.dma_start(out=out_1[kt * P : (kt + 1) * P, :], in_=db_rows[kt][:])
+            nc.vector.tensor_tensor(out=db_rows[d][:, j, cols], in0=bank[:], in1=db_rows[d][:, j, cols], op=ALU.add)
+            dst = out_1[2 * P * d : 2 * P * (d + 1), :].rearrange("(p j) n -> p j n", j=2)
+            if d in WHOLE:
+                if j == 1 and nh == 1:
+                    nc.sync.dma_start(out=dst, in_=db_rows[d][:])
+            elif d == 7 and j == 1:
+                nc.sync.dma_start(out=dst[:, j, cols], in_=db_rows[d][:, j, cols])
+            elif nh == 1:
+                nc.sync.dma_start(out=dst[:, j, :], in_=db_rows[d][:, j, :])
 
         ident = keep.tile([P, P], F32, name="ident")
         big = keep.tile([P, P], F32, name="big")
         diag = keep.tile([P, N], F32, name="diag")
-        shift = keep.tile([P, N], F32, name="shift")
+        shift = {}
 
-        g_raw, y_raw, b_raw, x_raw = [], [], {}, {}
         for grp in range(2):
-            g_raw.append(load("g%d" % grp, token_rows(grad_out, grp, 0)))
-            y_raw.append(load("y%d" % grp, token_rows(y, grp, 0), stage, "wide", WIDE_BUFS))
-        b_raw[0] = load("b0", beta_rows(0))
-        for kc in range(2):
-            for grp in range(2):
-                x_raw[kc, grp] = load("x%d%d" % (kc, grp), token_rows(x, grp, kc * BANK, BANK))
-            b_raw[kc + 1] = load("b%d" % (kc + 1), beta_rows(kc + 1))
-        b_raw[3] = load("b3", beta_rows(3))
-        for grp in range(2):
-            x_raw[2, grp] = load("x2%d" % grp, token_rows(x, grp, WIDE))
+            load_tokens(g_raw, "g", grad_out, grp)
+            load_tokens(y_raw, "y", y, grp)
+        for kind, a in LOADS:
+            if kind == "b":
+                load_beta(a)
+            else:
+                load_x(a, 0)
+                load_x(a, 1)
         make_identity(nc, ident[:])
         nc.vector.memset(big[:], 1.0 / STEP)
-
-        g_tok = [[None, None], [None, None]]
-        g_feat = [[None, None], [None, None]]
-        b_feat = [[None, None] for kc in range(4)]
-        x_tok = {}
-        x_grouped = {}
-
-        def g_tokens(grp):
-            inter = []
-            for nh in range(2):
-                inter.append(new_grouped("gi%d%d" % (grp, nh)))
-                interleave(nc.vector.tensor_copy, inter[nh][:], g_raw[grp][:, :, nh * BANK : (nh + 1) * BANK])
-            return inter
-
-        def g_tok_quant(grp, nh, grouped):
-            g_tok[nh][grp] = quantize("gtok%d%d" % (nh, grp), grouped, E5M2)
-
-        def g_turn(grp, nh):
-            return transposed("gt%d%d" % (grp, nh), g_raw[grp], nh)
-
-        def g_quant(grp, nh, turned):
-            g_feat[grp][nh] = quantize("gfeat%d%d" % (grp, nh), turned, E5M2)
-
-        def b_turn(kc, nh):
-            return transposed("bt%d%d" % (kc, nh), b_raw[kc], nh)
-
-        def b_quant(kc, nh, turned):
-            b_feat[kc][nh] = quantize("bfeat%d%d" % (kc, nh), turned, E4M3)
-
-        def x_inter(kt, grp, copy=nc.scalar.copy):
-            if grp == 0:
-                x_grouped[kt] = work.tile([P, 2 * BANK], BF16, name="xi%d" % kt, tag="xi", bufs=XI_BUFS, align_bytes=64)
-            part = min(kt // 4, 2)
-            t = kt - 4 * part
-            interleave(copy, x_grouped[kt][:, grp * BANK : (grp + 1) * BANK], x_raw[part, grp][:, :, t * P : (t + 1) * P])
-
-        def x_quant(kt):
-            x_tok[kt] = quantize("xtok%d" % kt, x_grouped[kt], E4M3)
-
-        zeros = keep.tile([P, BANK], BF16, name="zeros")
-        nc.vector.memset(zeros[:], 0.0)
-        warm = new_bank("warm", "vector")
+        warm = new_bank("warm", "shift")
+        ones = keep.tile([P, P], F32, name="ones")
+        nc.scalar.activation(out=ones[:], in_=big[:], func=ACT.Sign)
         for s in range(WARM):
-            nc.tensor.matmul(out=warm[:], lhsT=zeros[:, :P], rhs=zeros[:], start=True, stop=True)
+            nc.tensor.matmul(out=warm[:, :P], lhsT=big[:], rhs=big[:] if s < WARM - 1 else ones[:], start=True, stop=True)
 
         gy = [new_bank("gy%d" % nh, "vector") for nh in range(2)]
-        inter = g_tokens(0)
+        inter = [g_inter(0, nh, nc.vector.tensor_copy) for nh in range(2)]
         turned = [g_turn(0, nh) for nh in range(2)]
         for nh in range(2):
             g_tok_quant(0, nh, inter[nh])
+        gy_part(gy[0], 0, 0)
         for nh in range(2):
-            gy_part(gy[nh], nh, 0)
             g_quant(0, nh, turned[nh])
-        inter = g_tokens(1)
-        turned = [g_turn(1, nh) for nh in range(2)]
+        inter = [g_inter(1, nh, nc.scalar.copy if nh >= GI_VECTOR else nc.vector.tensor_copy) for nh in range(2)]
+        turned = []
+        for nh in range(2):
+            gy_part(gy[1], 1, 0, range(2 * nh, 2 * nh + 2))
+            turned.append(g_turn(1, nh))
         for nh in range(2):
             gy_part(gy[nh], nh, 1)
-        for nh in range(2):
-            g_quant(1, nh, turned[nh])
-            mask_half(nh, gy[nh])
-            spread_half(nh)
-            x_inter(0, nh)
+        g_quant(1, 0, turned[0])
         for nh in range(2):
             g_tok_quant(1, nh, inter[nh])
+        mask_half(0, gy[0])
+        g_quant(1, 1, turned[1])
+        mask_half(1, gy[1])
+        bt = []
+        for nh in range(2):
+            bt.append(b_turn(0, nh))
+            spread_half(nh)
         lift(0)
-        for unit in range(4):
-            kc, nh = divmod(unit, 2)
-            turned = b_turn(kc, nh)
-            if unit < 2 * (X_AHEAD - 1):
-                x_inter(1 + kc, nh)
-            lift(unit + 1)
-            if unit < AHEAD:
-                db_shift(unit)
-            b_quant(kc, nh, turned)
-            if nh == 0 and kc < X_AHEAD - 1:
-                x_quant(kc)
+        lift(1)
+        for nh in range(2):
+            b_quant(0, nh, bt[nh])
+            db_shift(0, nh)
+            if nh == 0:
+                db_shift(1, 0)
+        x_inter(0, 0)
+        bt = [b_turn(1, 0)]
+        dx_group(0)
+        dx_group(1)
+        x_inter(0, 1, nc.vector.tensor_copy if X01_VECTOR else nc.scalar.copy)
+        bt.append(b_turn(1, 1))
+        b_quant(1, 0, bt[0])
+        db_shift(1, 1)
+        dx_group(2)
+        dx_group(3)
+        lift(2)
+        if X_FIRST:
+            x_quant(0)
+        b_quant(1, 1, bt[1])
+        if not X_FIRST:
+            x_quant(0)
+        x_inter(1, 0)
+        x_inter(1, 1)
+        index = 4
+        for s in range(index, LEAD):
+            dx_group(index)
+            index = index + 1
 
+        quarters = [(d, j, nh) for d in range(8) for j in range(2) for nh in range(2)]
+        banks = {}
         turned = {}
-        index = 0
-        for kt in range(16):
-            turning = kt % 2 == TURN_ODD and kt < 8
-            banks = []
-            for nh in range(2):
-                banks.append(db_product(kt, nh))
-                if nh == 1 and turning:
-                    turned[kt] = b_turn(2 + kt // 4, kt // 2 % 2)
-                for s in range(2 if nh == 1 and not turning and kt >= FAST else 1):
-                    if index < 32:
-                        dx_group(index)
-                        index = index + 1
-                if kt + X_AHEAD < 16:
-                    x_inter(kt + X_AHEAD, nh)
-            if kt + AHEAD < 16:
-                db_shift(kt + AHEAD)
-            if kt + X_AHEAD - 1 < 16:
-                x_quant(kt + X_AHEAD - 1)
-            db_add(kt, 0, banks[0])
-            if kt + 5 < 16:
-                lift(kt + 5)
-            if kt - 1 in turned:
-                b_quant(2 + (kt - 1) // 4, (kt - 1) // 2 % 2, turned[kt - 1])
-            db_add(kt, 1, banks[1])
+        waiting = []
+        stores = {}
+        ready, unit, since, budget = 2, 4, SINCE, 0
+        for n in range(-DB_LEAD, 32):
+            d, q = divmod(n, 4)
+            if n - TURN_LAG in turned:
+                waiting.extend(turned[n - TURN_LAG])
+            if n >= 0 and q == 2:
+                if 3 <= d + LIFT_LEAD < 8 and d + LIFT_LEAD not in SIGN_PAIRS:
+                    lift(d + LIFT_LEAD)
+            if n >= 0 and q in QUANT_AT:
+                for item in waiting:
+                    b_quant(*item)
+                    ready = ready + 1
+                waiting = []
+            if n >= 0 and q == 2 and d + 1 < 8:
+                x_quant(d + 1)
+                if d + 2 < 8:
+                    x_inter(d + 2, 0)
+                    x_inter(d + 2, 1)
+            if q % 2 == 0 and 4 <= n // 2 + SHIFT_LEAD < 16:
+                db_shift(*divmod(n // 2 + SHIFT_LEAD, 2))
+            if n + DB_LEAD < 32:
+                banks[n + DB_LEAD] = db_product(*quarters[n + DB_LEAD])
+            budget = budget + FILL_NUM
+            while budget >= FILL_DEN:
+                unlocked = index < (FIRST[0], 16, 16 + FIRST[1], 32)[min(3, ready // 2)]
+                if unit < 8 and (since >= DX_PER_TURN or not unlocked):
+                    turned.setdefault(n, []).append((unit // 2, unit % 2, b_turn(unit // 2, unit % 2)))
+                    unit, since, budget = unit + 1, 0, budget - 2 * FILL_DEN
+                elif unlocked and index < 32:
+                    dx_group(index)
+                    index, since, budget = index + 1, since + 1, budget - FILL_DEN
+                else:
+                    budget = 0
+            stores[n + STORE_LAG] = list(dx_done)
+            dx_done.clear()
+            for dst, src in stores.get(n, []):
+                nc.sync.dma_start(out=dst, in_=src)
+            if (n + SIGN_LEAD) // 4 in SIGN_PAIRS:
+                sign(*divmod(n + SIGN_LEAD, 4))
+            if n >= 0:
+                db_add(*quarters[n], banks[n])
+        assert index == 32 and not any(stores[n] for n in stores if n >= 32)

@@ -24,13 +24,13 @@ BANK = 512
 WIDE = 1024
 LIFT = 2.0**100
 STEP = 2.0**-33
-GROUPED_BUFS = 3
+GROUPED_BUFS = 4
 XI_BUFS = 2
 X_AHEAD = 2
 AHEAD = 2
 WIDE_BUFS = 8
 WARM = 12
-POOL_FROM = 1
+POOL_FROM = 8
 XI_AT = 4
 LEAD = 6
 X_CUTS = [0, 1024, 2048]
@@ -39,7 +39,7 @@ DX_RATE = [3, 3, 3, 3, 4, 5, 5, 5]
 DB_LEAD = 2
 ORDER = [0, 2, 1, 3]
 TURN_AT = [-2, -1, 2, 4, 6, 8]
-TURN_LAG = 3
+TURN_LAG = 4
 DX_NUM = 9
 DX_DEN = 8
 X_LEAD = 8
@@ -49,12 +49,12 @@ SHIFT_LEAD = 4
 LIFT_LEAD = 3
 FIRST = [4, 0]
 G11_FIRST = False
-BANKS = {"vector": 3, "scalar": 3, "shift": 2}
-SIGN_PAIRS = [3, 4, 5, 6, 7]
+BANKS = {"vector": 3, "scalar": 4, "shift": 1}
+SIGN_PAIRS = []
 SIGN_AT = [0, 1]
-LIFT_BUFS = 4
+LIFT_BUFS = 2
 QUANT_AT = [2]
-XP_BUFS = 1
+XP_BUFS = 4
 STORE_LAG = 2
 GI_VECTOR = 2
 FILL_NUM = 3
@@ -65,6 +65,12 @@ X01_VECTOR = True
 X_FIRST = False
 WHOLE = []
 SIGN_LEAD = 14
+POOL_GROUPS = 0
+XS_LEAD = 9
+XS_AT = [0, 2]
+POOL_PAIRS = [2, 3, 4, 5, 6, 7]
+VX_PAIRS = [1, 3, 5, 7]
+KEEP = 2
 
 
 def tile_advresnet_v_kernel(
@@ -158,7 +164,7 @@ def tile_advresnet_v_kernel(
         x_tok, x_grouped, dx_rows, db_rows, lifted = {}, {}, {}, {}, {}
 
         def g_inter(grp, nh, copy):
-            grouped = work.tile([P, BANK * PACK], BF16, name="gi%d%d" % (grp, nh), tag="xi", bufs=XI_BUFS, align_bytes=64)
+            grouped = work.tile([P, BANK * PACK], BF16, name="gi%d%d" % (grp, nh), tag="xp", bufs=XP_BUFS, align_bytes=64)
             copy(
                 out=grouped[:].rearrange("p (c i t) -> p c t i", i=4, t=PACK),
                 in_=g_raw[grp][:, :, nh * BANK : (nh + 1) * BANK].rearrange("p t (c i) -> p c t i", i=4),
@@ -181,7 +187,7 @@ def tile_advresnet_v_kernel(
             b_feat[kc][nh] = quantize("bfeat%d%d" % (kc, nh), turned, E4M3)
 
         def x_inter(d, grp, copy=nc.scalar.copy):
-            on_pool = d >= POOL_FROM
+            on_pool = d >= POOL_FROM and grp < POOL_GROUPS
             if grp == 0:
                 tag, bufs = ("xp", XP_BUFS)
                 x_grouped[d] = work.tile([P, BANK * PACK], BF16, name="xi%d" % d, tag=tag, bufs=bufs, align_bytes=64)
@@ -255,8 +261,12 @@ def tile_advresnet_v_kernel(
             )
 
         def spread_half(nh):
-            shift[nh] = new_bank("shift%d" % nh, "shift")
-            nc.tensor.matmul(out=shift[nh][:], lhsT=big[:], rhs=diag[:, nh * BANK : (nh + 1) * BANK], start=True, stop=True)
+            bank = new_bank("shift%d" % nh, "shift" if nh == 0 else "scalar")
+            nc.tensor.matmul(out=bank[:], lhsT=big[:], rhs=diag[:, nh * BANK : (nh + 1) * BANK], start=True, stop=True)
+            shift[nh] = bank
+            if nh == 1:
+                shift[nh] = keep.tile([P, BANK], F32, name="shift_high")
+                nc.scalar.copy(out=shift[nh][:], in_=bank[:])
 
         def lift(d):
             kc, side = divmod(d, 2)
@@ -278,6 +288,16 @@ def tile_advresnet_v_kernel(
             if nh == 0:
                 db_rows[d] = wide.tile([P, 2, N], F32, name="db%d" % d, tag="wide", align_bytes=64)
             cols = slice(nh * BANK, (nh + 1) * BANK)
+            if nh == 1 and d in POOL_PAIRS:
+                signs = work.tile([P, 2, BANK], BF16, name="signs%d" % d, tag="signs", bufs=1)
+                nc.vector.tensor_single_scalar(out=signs[:], in_=lifted[d][:, :, cols], scalar=STEP, op=ALU.min)
+                nc.gpsimd.tensor_tensor(
+                    out=db_rows[d][:, :, cols],
+                    in0=signs[:],
+                    in1=shift[nh][:].unsqueeze(1).to_broadcast([P, 2, BANK]),
+                    op=ALU.mult,
+                )
+                return
             nc.vector.scalar_tensor_tensor(
                 out=db_rows[d][:, :, cols],
                 in0=lifted[d][:, :, cols],
@@ -319,10 +339,8 @@ def tile_advresnet_v_kernel(
         make_identity(nc, ident[:])
         nc.vector.memset(big[:], 1.0 / STEP)
         warm = new_bank("warm", "shift")
-        ones = keep.tile([P, P], F32, name="ones")
-        nc.scalar.activation(out=ones[:], in_=big[:], func=ACT.Sign)
         for s in range(WARM):
-            nc.tensor.matmul(out=warm[:, :P], lhsT=big[:], rhs=big[:] if s < WARM - 1 else ones[:], start=True, stop=True)
+            nc.tensor.matmul(out=warm[:, :P], lhsT=big[:], rhs=big[:], start=True, stop=True)
 
         gy = [new_bank("gy%d" % nh, "vector") for nh in range(2)]
         inter = [g_inter(0, nh, nc.vector.tensor_copy) for nh in range(2)]
@@ -373,7 +391,7 @@ def tile_advresnet_v_kernel(
         if not X_FIRST:
             x_quant(0)
         x_inter(1, 0)
-        x_inter(1, 1)
+        x_inter(1, 1, nc.vector.tensor_copy if 1 in VX_PAIRS else nc.scalar.copy)
         index = 4
         for s in range(index, LEAD):
             dx_group(index)
@@ -399,9 +417,11 @@ def tile_advresnet_v_kernel(
                 waiting = []
             if n >= 0 and q == 2 and d + 1 < 8:
                 x_quant(d + 1)
+                if d + 2 in VX_PAIRS:
+                    x_inter(d + 2, 1, nc.vector.tensor_copy)
                 if d + 2 < 8:
-                    x_inter(d + 2, 0)
-                    x_inter(d + 2, 1)
+                    for grp in range(POOL_GROUPS):
+                        x_inter(d + 2, grp)
             if q % 2 == 0 and 4 <= n // 2 + SHIFT_LEAD < 16:
                 db_shift(*divmod(n // 2 + SHIFT_LEAD, 2))
             if n + DB_LEAD < 32:
@@ -417,6 +437,9 @@ def tile_advresnet_v_kernel(
                     index, since, budget = index + 1, since + 1, budget - FILL_DEN
                 else:
                     budget = 0
+            xd, xq = divmod(n + XS_LEAD, 4)
+            if 2 <= xd < 8 and xq in XS_AT[POOL_GROUPS:] and not (xd in VX_PAIRS and xq == XS_AT[1]):
+                x_inter(xd, XS_AT.index(xq))
             stores[n + STORE_LAG] = list(dx_done)
             dx_done.clear()
             for dst, src in stores.get(n, []):

@@ -15,62 +15,31 @@ U8 = mybir.dt.uint8
 E4M3 = mybir.dt.float8_e4m3fn_x4
 E5M2 = mybir.dt.float8_e5m2_x4
 ALU = mybir.AluOpType
-ACT = mybir.ActivationFunctionType
 
 P = 128
 PACK = 4
 PASS = P * PACK
 BANK = 512
-WIDE = 1024
+HALF_K = K // 2
+PAIR = 2 * P
+PAIRS = K // PAIR
+DX_BANKS = (B // P) * (K // BANK)
+DB_BANKS = (K // P) * (N // BANK)
+
 LIFT = 2.0**100
 STEP = 2.0**-33
-GROUPED_BUFS = 4
-XI_BUFS = 2
-X_AHEAD = 2
-AHEAD = 2
-WIDE_BUFS = 8
-WARM = 12
-POOL_FROM = 8
-XI_AT = 4
-LEAD = 6
-X_CUTS = [0, 1024, 2048]
-LOADS = [("b", 0), ("b", 1), ("x", 0), ("b", 2), ("b", 3), ("x", 1)]
-DX_RATE = [3, 3, 3, 3, 4, 5, 5, 5]
-DB_LEAD = 2
-ORDER = [0, 2, 1, 3]
-TURN_AT = [-2, -1, 2, 4, 6, 8]
-TURN_LAG = 4
-DX_NUM = 9
-DX_DEN = 8
-X_LEAD = 8
-BT1_AT = [0, 1]
-XQ_AT = 2
-SHIFT_LEAD = 4
-LIFT_LEAD = 3
-FIRST = [4, 0]
-G11_FIRST = False
+
 BANKS = {"vector": 3, "scalar": 4, "shift": 1}
-SIGN_PAIRS = []
-SIGN_AT = [0, 1]
-LIFT_BUFS = 2
-QUANT_AT = [2]
-XP_BUFS = 4
-STORE_LAG = 2
-GI_VECTOR = 2
-FILL_NUM = 3
-FILL_DEN = 2
-DX_PER_TURN = 1
-SINCE = 0
-X01_VECTOR = True
-X_FIRST = False
-WHOLE = []
-SIGN_LEAD = 14
-POOL_GROUPS = 0
-XS_LEAD = 9
-XS_AT = [0, 2]
-POOL_PAIRS = [2, 3, 4, 5, 6, 7]
-VX_PAIRS = [1, 3, 5, 7]
-KEEP = 2
+WIDE_BUFS = 8
+TURNED_BUFS = 4
+INTERLEAVED_BUFS = 4
+
+DB_LEAD = BANKS["vector"] - 1
+SHIFT_LEAD = 4
+LIFT_LEAD = SHIFT_LEAD // 2 + 1
+INTERLEAVE_LEAD = 9
+DX_BEFORE = 6
+POOL_FROM = 2
 
 
 def tile_advresnet_v_kernel(
@@ -85,174 +54,161 @@ def tile_advresnet_v_kernel(
         psum = ctx.enter_context(tc.psum_pool(name="psum", bufs=1))
         ctx.enter_context(tc.manual_schedule())
 
-        def token_rows(src, grp, c0, width):
-            return src[grp * PASS : (grp + 1) * PASS, c0 : c0 + width].rearrange("(p j) w -> p j w", j=PACK)
-
         g_raw, y_raw, b_raw, x_raw = {}, {}, {}, {}
+        g_tok = [[None, None], [None, None]]
+        g_feat = [[None, None], [None, None]]
+        b_feat = [[None, None] for kc in range(K // BANK)]
+        x_tok, x_mixed, dx_rows, db_rows, lifted, shift = {}, {}, {}, {}, {}, {}
+        dx_ready = []
 
-        def load_tokens(store, name, src, grp):
-            store[grp] = wide.tile([P, PACK, N], BF16, name="%s%d" % (name, grp), tag="wide", align_bytes=64)
-            nc.sync.dma_start(out=store[grp][:], in_=token_rows(src, grp, 0, N))
+        def half(nh):
+            return slice(nh * BANK, (nh + 1) * BANK)
+
+        def token_rows(src, grp, cols):
+            return src[grp * PASS : (grp + 1) * PASS, cols].rearrange("(p s) w -> p s w", s=PACK)
+
+        def load_tokens(tiles, name, src, grp):
+            tiles[grp] = wide.tile([P, PACK, N], BF16, name="%s%d" % (name, grp), tag="wide", align_bytes=64)
+            nc.sync.dma_start(out=tiles[grp][:], in_=token_rows(src, grp, slice(0, N)))
 
         def load_beta(kc):
             b_raw[kc] = keep.tile([P, PACK, N], BF16, name="b%d" % kc, align_bytes=64)
             nc.sync.dma_start(
-                out=b_raw[kc][:].rearrange("p (d j) n -> p d (j n)", j=2),
-                in_=beta[kc * BANK : (kc + 1) * BANK, :].rearrange("(d p j) n -> p d (j n)", p=P, j=2),
+                out=b_raw[kc][:].rearrange("p (e j) n -> p e (j n)", j=2),
+                in_=beta[kc * BANK : (kc + 1) * BANK, :].rearrange("(e p j) n -> p e (j n)", p=P, j=2),
             )
 
-        def load_x(part, grp):
-            c0, c1 = X_CUTS[part], X_CUTS[part + 1]
-            x_raw[part, grp] = keep.tile([P, PACK, c1 - c0], BF16, name="x%d%d" % (part, grp))
-            nc.sync.dma_start(out=x_raw[part, grp][:], in_=token_rows(x, grp, c0, c1 - c0))
+        def load_x(kh):
+            for grp in range(2):
+                x_raw[kh, grp] = keep.tile([P, PACK, HALF_K], BF16, name="x%d%d" % (kh, grp))
+                cols = slice(kh * HALF_K, (kh + 1) * HALF_K)
+                nc.sync.dma_start(out=x_raw[kh, grp][:], in_=token_rows(x, grp, cols))
 
         def new_bank(name, reader):
             bank = psum.tile([P, BANK], F32, name=name, tag=reader, bufs=BANKS[reader])
             return bank
 
-        def new_grouped(name):
-            grouped = work.tile([P, BANK * PACK], BF16, name=name, tag="grouped", bufs=GROUPED_BUFS, align_bytes=64)
-            return grouped
+        def new_interleaved(name):
+            mixed = work.tile([P, BANK * PACK], BF16, name=name, tag="mixed", bufs=INTERLEAVED_BUFS, align_bytes=64)
+            return mixed
 
-        def transposed(name, raw, grp):
+        def turn(name, raw, nh):
             words = raw[:].bitcast(F32)
-            w0 = grp * PASS // 2
+            w0 = nh * PASS // 2
             banks = []
-            for pair in range(2):
-                banks.append(new_bank("%s_ps%d" % (name, pair), "scalar"))
+            for two in range(2):
+                banks.append(new_bank("%s_ps%d" % (name, two), "scalar"))
                 for a in range(2):
                     for u in range(2):
                         c0 = (2 * a + u) * P
                         nc.tensor.transpose(
-                            banks[pair][:, c0 : c0 + P], words[:, 2 * pair + a, w0 + u : w0 + PASS // 2 : 2], ident[:]
+                            banks[two][:, c0 : c0 + P], words[:, 2 * two + a, w0 + u : w0 + PASS // 2 : 2], ident[:]
                         )
-            grouped = new_grouped(name)
-            for pair in range(2):
-                dst = grouped[:].bitcast(F32)[:, pair * BANK : (pair + 1) * BANK]
+            turned = work.tile([P, BANK * PACK], BF16, name=name, tag="turned", bufs=TURNED_BUFS, align_bytes=64)
+            for two in range(2):
+                dst = turned[:].bitcast(F32)[:, two * BANK : (two + 1) * BANK]
                 nc.scalar.copy(
-                    out=dst.rearrange("p (a r u) -> p a r u", a=2, u=2),
-                    in_=banks[pair][:].rearrange("p (a u r) -> p a r u", a=2, u=2),
+                    out=dst.rearrange("p (a c u) -> p a c u", a=2, u=2),
+                    in_=banks[two][:].rearrange("p (a u c) -> p a c u", a=2, u=2),
                 )
-            return grouped
+            return turned
 
-        def quantize(name, grouped, fmt):
+        def quantize(name, values, fmt):
             codes = keep.tile([P, BANK], U32, name=name + "_codes", align_bytes=64)
             scales = keep.tile([P, BANK], U8, name=name + "_scales", align_bytes=64)
-            nc.vector.quantize_mx(out=codes[:].bitcast(fmt), scales=scales[:], in_=grouped[:])
+            nc.vector.quantize_mx(out=codes[:].bitcast(fmt), scales=scales[:], in_=values[:])
             return codes, scales, fmt
 
         def product(name, reader, stationary, moving):
             bank = new_bank(name, reader)
-            for grp in range(2):
-                (lc, ls, lf), m = stationary[grp]
+            for g in range(2):
+                (l_codes, l_scales, l_fmt), m = stationary[g]
                 cols = slice(m * P, (m + 1) * P)
-                rc, rs, rf = moving[grp]
+                r_codes, r_scales, r_fmt = moving[g]
                 nc.tensor.matmul_mx(
                     out=bank[:],
-                    lhsT=lc[:, cols].bitcast(lf),
-                    lhsT_scale=ls[:, cols],
-                    rhs=rc[:].bitcast(rf),
-                    rhs_scale=rs[:],
-                    start=(grp == 0),
-                    stop=(grp == 1),
+                    lhsT=l_codes[:, cols].bitcast(l_fmt),
+                    lhsT_scale=l_scales[:, cols],
+                    rhs=r_codes[:].bitcast(r_fmt),
+                    rhs_scale=r_scales[:],
+                    start=(g == 0),
+                    stop=(g == 1),
                 )
             return bank
 
-        g_tok = [[None, None], [None, None]]
-        g_feat = [[None, None], [None, None]]
-        b_feat = [[None, None] for kc in range(4)]
-        x_tok, x_grouped, dx_rows, db_rows, lifted = {}, {}, {}, {}, {}
-
-        def g_inter(grp, nh, copy):
-            grouped = work.tile([P, BANK * PACK], BF16, name="gi%d%d" % (grp, nh), tag="xp", bufs=XP_BUFS, align_bytes=64)
-            copy(
-                out=grouped[:].rearrange("p (c i t) -> p c t i", i=4, t=PACK),
-                in_=g_raw[grp][:, :, nh * BANK : (nh + 1) * BANK].rearrange("p t (c i) -> p c t i", i=4),
+        def g_interleave(grp, nh):
+            mixed = new_interleaved("gi%d%d" % (grp, nh))
+            nc.vector.tensor_copy(
+                out=mixed[:].rearrange("p (c i s) -> p c s i", i=4, s=PACK),
+                in_=g_raw[grp][:, :, half(nh)].rearrange("p s (c i) -> p c s i", i=4),
             )
-            return grouped
+            return mixed
 
-        def g_tok_quant(grp, nh, grouped):
-            g_tok[nh][grp] = quantize("gtok%d%d" % (nh, grp), grouped, E5M2)
+        def g_tok_quantize(grp, nh, mixed):
+            g_tok[nh][grp] = quantize("gtok%d%d" % (nh, grp), mixed, E5M2)
 
         def g_turn(grp, nh):
-            return transposed("gt%d%d" % (grp, nh), g_raw[grp], nh)
+            return turn("gt%d%d" % (grp, nh), g_raw[grp], nh)
 
-        def g_quant(grp, nh, turned):
+        def g_feat_quantize(grp, nh, turned):
             g_feat[grp][nh] = quantize("gfeat%d%d" % (grp, nh), turned, E5M2)
 
         def b_turn(kc, nh):
-            return transposed("bt%d%d" % (kc, nh), b_raw[kc], nh)
+            return turn("bt%d%d" % (kc, nh), b_raw[kc], nh)
 
-        def b_quant(kc, nh, turned):
+        def b_quantize(kc, nh, turned):
             b_feat[kc][nh] = quantize("bfeat%d%d" % (kc, nh), turned, E4M3)
 
-        def x_inter(d, grp, copy=nc.scalar.copy):
-            on_pool = d >= POOL_FROM and grp < POOL_GROUPS
+        def x_interleave(d, grp, copy):
             if grp == 0:
-                tag, bufs = ("xp", XP_BUFS)
-                x_grouped[d] = work.tile([P, BANK * PACK], BF16, name="xi%d" % d, tag=tag, bufs=bufs, align_bytes=64)
-            part = max(s for s in range(len(X_CUTS) - 1) if X_CUTS[s] <= 2 * P * d)
-            c0 = 2 * P * d - X_CUTS[part]
-            dst = x_grouped[d][:, grp * 2 * BANK : (grp + 1) * 2 * BANK]
-            src = x_raw[part, grp][:, :, c0 : c0 + 2 * P]
-            if on_pool:
-                nc.gpsimd.tensor_scalar(
-                    out=dst.rearrange("p (j m t) -> p j m t", j=2, t=PACK),
-                    in0=src.rearrange("p t (m j) -> p j m t", j=2),
-                    scalar1=1.0,
-                    scalar2=0.0,
-                    op0=ALU.mult,
-                    op1=ALU.add,
-                )
-            else:
-                copy(
-                    out=dst.rearrange("p (j c m t) -> p c t m j", j=2, m=2, t=PACK),
-                    in_=src.rearrange("p t (c m j) -> p c t m j", m=2, j=2),
-                )
+                x_mixed[d] = new_interleaved("xi%d" % d)
+            kh, c0 = divmod(d * PAIR, HALF_K)
+            dst = x_mixed[d][:, grp * PAIR * PACK : (grp + 1) * PAIR * PACK]
+            copy(
+                out=dst.rearrange("p (j c m s) -> p c s m j", j=2, m=2, s=PACK),
+                in_=x_raw[kh, grp][:, :, c0 : c0 + PAIR].rearrange("p s (c m j) -> p c s m j", m=2, j=2),
+            )
 
-        def x_quant(d):
-            x_tok[d] = quantize("xtok%d" % d, x_grouped[d], E4M3)
+        def x_quantize(d):
+            x_tok[d] = quantize("xtok%d" % d, x_mixed[d], E4M3)
 
-        dx_done = []
+        dx_order = [(0, s, kc) for kc in range(2) for s in range(PACK)]
+        dx_order = dx_order + [(1, s, kc) for s in range(PACK) for kc in range(2)]
+        dx_order = dx_order + [(grp, s, kc) for grp in range(2) for s in range(PACK) for kc in range(2, 4)]
 
-        def dx_group(index):
-            half, rest = divmod(index, 16)
-            if rest < 2 * FIRST[half]:
-                side, rest = divmod(rest, FIRST[half])
-            else:
-                rest, side = divmod(rest, 2)
-            grp, j = divmod(rest, PACK)
-            pair, a = divmod(j, 2)
-            kc = 2 * half + side
+        def dx_bank(index):
+            grp, s, kc = dx_order[index]
+            kh, side = divmod(kc, 2)
+            two, a = divmod(s, 2)
             if side == 0 and a == 0:
-                dx_rows[grp, pair] = wide.tile(
-                    [P, 2, WIDE], F32, name="dx%d%d%d" % (grp, pair, half), tag="wide", align_bytes=64
-                )
-            rows = dx_rows[grp, pair]
-            bank = product("dx_ps%d%d%d" % (grp, j, kc), "scalar", [(g_feat[grp][nh], j) for nh in range(2)], b_feat[kc])
+                name = "dx%d%d%d" % (grp, two, kh)
+                dx_rows[grp, two] = wide.tile([P, 2, HALF_K], F32, name=name, tag="wide", align_bytes=64)
+            rows = dx_rows[grp, two]
+            stationary = [(g_feat[grp][nh], s) for nh in range(2)]
+            bank = product("dx_ps%d%d%d" % (grp, s, kc), "scalar", stationary, b_feat[kc])
             nc.scalar.copy(
-                out=rows[:, a, side * BANK : (side + 1) * BANK].rearrange("p (d r j) -> p d r j", d=2, j=2),
-                in_=bank[:].rearrange("p (d j r) -> p d r j", d=2, j=2),
+                out=rows[:, a, half(side)].rearrange("p (e c j) -> p e c j", e=2, j=2),
+                in_=bank[:].rearrange("p (e j c) -> p e c j", e=2, j=2),
             )
             if side == 1:
-                dst = out_0[grp * PASS : (grp + 1) * PASS, half * WIDE : (half + 1) * WIDE]
-                dx_done.append((dst.rearrange("(p j) k -> p j k", j=PACK)[:, j, :], rows[:, a, :]))
+                dst = token_rows(out_0, grp, slice(kh * HALF_K, (kh + 1) * HALF_K))
+                dx_ready.append((dst[:, s, :], rows[:, a, :]))
 
-        def gy_part(bank, nh, grp, blocks=range(4)):
+        def gy_blocks(bank, nh, grp, blocks):
             for q in blocks:
                 cols = slice(nh * BANK + q * P, nh * BANK + (q + 1) * P)
-                for j in range(PACK):
+                for s in range(PACK):
                     nc.tensor.matmul(
                         out=bank[:, q * P : (q + 1) * P],
-                        lhsT=g_raw[grp][:, j, cols],
-                        rhs=y_raw[grp][:, j, cols],
-                        start=(grp == 0 and q == 0 and j == 0),
-                        stop=(grp == 1 and q == 3 and j == PACK - 1),
+                        lhsT=g_raw[grp][:, s, cols],
+                        rhs=y_raw[grp][:, s, cols],
+                        start=(grp == 0 and q == 0 and s == 0),
+                        stop=(grp == 1 and q == 3 and s == PACK - 1),
                     )
 
-        def mask_half(nh, bank):
+        def keep_diagonal(nh, bank):
             nc.vector.scalar_tensor_tensor(
-                out=diag[:, nh * BANK : (nh + 1) * BANK].rearrange("p (q c) -> p q c", q=4),
+                out=diag[:, half(nh)].rearrange("p (q c) -> p q c", q=4),
                 in0=bank[:].rearrange("p (q c) -> p q c", q=4),
                 scalar=-EPSILON,
                 in1=ident[:].unsqueeze(1).to_broadcast([P, 4, P]),
@@ -260,192 +216,156 @@ def tile_advresnet_v_kernel(
                 op1=ALU.mult,
             )
 
-        def spread_half(nh):
+        def spread_shift(nh):
             bank = new_bank("shift%d" % nh, "shift" if nh == 0 else "scalar")
-            nc.tensor.matmul(out=bank[:], lhsT=big[:], rhs=diag[:, nh * BANK : (nh + 1) * BANK], start=True, stop=True)
+            nc.tensor.matmul(out=bank[:], lhsT=inv_step[:], rhs=diag[:, half(nh)], start=True, stop=True)
             shift[nh] = bank
             if nh == 1:
                 shift[nh] = keep.tile([P, BANK], F32, name="shift_high")
                 nc.scalar.copy(out=shift[nh][:], in_=bank[:])
 
         def lift(d):
-            kc, side = divmod(d, 2)
-            lifted[d] = work.tile([P, 2, N], BF16, name="lifted%d" % d, tag="lifted", bufs=LIFT_BUFS)
-            dst = lifted[d][:].rearrange("p j n -> p (j n)")
-            src = b_raw[kc][:, 2 * side : 2 * side + 2, :].rearrange("p j n -> p (j n)")
-            if d not in SIGN_PAIRS:
-                nc.vector.tensor_scalar(out=dst, in0=src, scalar1=LIFT, scalar2=-STEP, op0=ALU.mult, op1=ALU.max)
-
-        def sign(d, q):
-            kc, side = divmod(d, 2)
-            j, nh = divmod(q, 2)
-            if q == 0:
-                lifted[d] = work.tile([P, 2, N], BF16, name="lifted%d" % d, tag="lifted", bufs=LIFT_BUFS)
-            cols = slice(nh * BANK, (nh + 1) * BANK)
-            nc.scalar.activation(out=lifted[d][:, j, cols], in_=b_raw[kc][:, 2 * side + j, cols], func=ACT.Sign)
+            kc, e = divmod(d, 2)
+            lifted[d] = work.tile([P, 2, N], BF16, name="lifted%d" % d, tag="lifted", bufs=2)
+            nc.vector.tensor_scalar(
+                out=lifted[d][:].rearrange("p j n -> p (j n)"),
+                in0=b_raw[kc][:, 2 * e : 2 * e + 2, :].rearrange("p j n -> p (j n)"),
+                scalar1=LIFT,
+                scalar2=-STEP,
+                op0=ALU.mult,
+                op1=ALU.max,
+            )
 
         def db_shift(d, nh):
             if nh == 0:
                 db_rows[d] = wide.tile([P, 2, N], F32, name="db%d" % d, tag="wide", align_bytes=64)
-            cols = slice(nh * BANK, (nh + 1) * BANK)
-            if nh == 1 and d in POOL_PAIRS:
+            row = shift[nh][:].unsqueeze(1).to_broadcast([P, 2, BANK])
+            if nh == 1 and d >= POOL_FROM:
                 signs = work.tile([P, 2, BANK], BF16, name="signs%d" % d, tag="signs", bufs=1)
-                nc.vector.tensor_single_scalar(out=signs[:], in_=lifted[d][:, :, cols], scalar=STEP, op=ALU.min)
-                nc.gpsimd.tensor_tensor(
-                    out=db_rows[d][:, :, cols],
-                    in0=signs[:],
-                    in1=shift[nh][:].unsqueeze(1).to_broadcast([P, 2, BANK]),
-                    op=ALU.mult,
+                nc.vector.tensor_single_scalar(out=signs[:], in_=lifted[d][:, :, half(nh)], scalar=STEP, op=ALU.min)
+                nc.gpsimd.tensor_tensor(out=db_rows[d][:, :, half(nh)], in0=signs[:], in1=row, op=ALU.mult)
+            else:
+                nc.vector.scalar_tensor_tensor(
+                    out=db_rows[d][:, :, half(nh)],
+                    in0=lifted[d][:, :, half(nh)],
+                    scalar=STEP,
+                    in1=row,
+                    op0=ALU.min,
+                    op1=ALU.mult,
                 )
-                return
-            nc.vector.scalar_tensor_tensor(
-                out=db_rows[d][:, :, cols],
-                in0=lifted[d][:, :, cols],
-                scalar=STEP,
-                in1=shift[nh][:].unsqueeze(1).to_broadcast([P, 2, BANK]),
-                op0=ALU.mult if d in SIGN_PAIRS else ALU.min,
-                op1=ALU.mult,
-            )
 
         def db_product(d, j, nh):
-            return product("db_ps%d%d%d" % (d, j, nh), "vector", [(x_tok[d], 2 * grp + j) for grp in range(2)], g_tok[nh])
+            stationary = [(x_tok[d], 2 * grp + j) for grp in range(2)]
+            return product("db_ps%d%d%d" % (d, j, nh), "vector", stationary, g_tok[nh])
 
         def db_add(d, j, nh, bank):
-            cols = slice(nh * BANK, (nh + 1) * BANK)
-            nc.vector.tensor_tensor(out=db_rows[d][:, j, cols], in0=bank[:], in1=db_rows[d][:, j, cols], op=ALU.add)
-            dst = out_1[2 * P * d : 2 * P * (d + 1), :].rearrange("(p j) n -> p j n", j=2)
-            if d in WHOLE:
-                if j == 1 and nh == 1:
-                    nc.sync.dma_start(out=dst, in_=db_rows[d][:])
-            elif d == 7 and j == 1:
-                nc.sync.dma_start(out=dst[:, j, cols], in_=db_rows[d][:, j, cols])
+            rows = db_rows[d]
+            nc.vector.tensor_tensor(out=rows[:, j, half(nh)], in0=bank[:], in1=rows[:, j, half(nh)], op=ALU.add)
+            dst = out_1[d * PAIR : (d + 1) * PAIR, :].rearrange("(p j) n -> p j n", j=2)
+            if d == PAIRS - 1 and j == 1:
+                nc.sync.dma_start(out=dst[:, j, half(nh)], in_=rows[:, j, half(nh)])
             elif nh == 1:
-                nc.sync.dma_start(out=dst[:, j, :], in_=db_rows[d][:, j, :])
+                nc.sync.dma_start(out=dst[:, j, :], in_=rows[:, j, :])
 
         ident = keep.tile([P, P], F32, name="ident")
-        big = keep.tile([P, P], F32, name="big")
+        inv_step = keep.tile([P, P], F32, name="inv_step")
         diag = keep.tile([P, N], F32, name="diag")
-        shift = {}
 
         for grp in range(2):
             load_tokens(g_raw, "g", grad_out, grp)
             load_tokens(y_raw, "y", y, grp)
-        for kind, a in LOADS:
-            if kind == "b":
-                load_beta(a)
-            else:
-                load_x(a, 0)
-                load_x(a, 1)
+        for kh in range(2):
+            load_beta(2 * kh)
+            load_beta(2 * kh + 1)
+            load_x(kh)
         make_identity(nc, ident[:])
-        nc.vector.memset(big[:], 1.0 / STEP)
-        warm = new_bank("warm", "shift")
-        for s in range(WARM):
-            nc.tensor.matmul(out=warm[:, :P], lhsT=big[:], rhs=big[:], start=True, stop=True)
+        nc.vector.memset(inv_step[:], 1.0 / STEP)
 
         gy = [new_bank("gy%d" % nh, "vector") for nh in range(2)]
-        inter = [g_inter(0, nh, nc.vector.tensor_copy) for nh in range(2)]
+        mixed = [g_interleave(0, nh) for nh in range(2)]
         turned = [g_turn(0, nh) for nh in range(2)]
         for nh in range(2):
-            g_tok_quant(0, nh, inter[nh])
-        gy_part(gy[0], 0, 0)
+            g_tok_quantize(0, nh, mixed[nh])
+        gy_blocks(gy[0], 0, 0, range(4))
         for nh in range(2):
-            g_quant(0, nh, turned[nh])
-        inter = [g_inter(1, nh, nc.scalar.copy if nh >= GI_VECTOR else nc.vector.tensor_copy) for nh in range(2)]
+            g_feat_quantize(0, nh, turned[nh])
+        mixed = [g_interleave(1, nh) for nh in range(2)]
         turned = []
         for nh in range(2):
-            gy_part(gy[1], 1, 0, range(2 * nh, 2 * nh + 2))
+            gy_blocks(gy[1], 1, 0, range(2 * nh, 2 * nh + 2))
             turned.append(g_turn(1, nh))
         for nh in range(2):
-            gy_part(gy[nh], nh, 1)
-        g_quant(1, 0, turned[0])
+            gy_blocks(gy[nh], nh, 1, range(4))
+        g_feat_quantize(1, 0, turned[0])
         for nh in range(2):
-            g_tok_quant(1, nh, inter[nh])
-        mask_half(0, gy[0])
-        g_quant(1, 1, turned[1])
-        mask_half(1, gy[1])
-        bt = []
+            g_tok_quantize(1, nh, mixed[nh])
+        keep_diagonal(0, gy[0])
+        g_feat_quantize(1, 1, turned[1])
+        keep_diagonal(1, gy[1])
+
+        turned = []
         for nh in range(2):
-            bt.append(b_turn(0, nh))
-            spread_half(nh)
+            turned.append(b_turn(0, nh))
+            spread_shift(nh)
         lift(0)
         lift(1)
-        for nh in range(2):
-            b_quant(0, nh, bt[nh])
-            db_shift(0, nh)
-            if nh == 0:
-                db_shift(1, 0)
-        x_inter(0, 0)
-        bt = [b_turn(1, 0)]
-        dx_group(0)
-        dx_group(1)
-        x_inter(0, 1, nc.vector.tensor_copy if X01_VECTOR else nc.scalar.copy)
-        bt.append(b_turn(1, 1))
-        b_quant(1, 0, bt[0])
-        db_shift(1, 1)
-        dx_group(2)
-        dx_group(3)
-        lift(2)
-        if X_FIRST:
-            x_quant(0)
-        b_quant(1, 1, bt[1])
-        if not X_FIRST:
-            x_quant(0)
-        x_inter(1, 0)
-        x_inter(1, 1, nc.vector.tensor_copy if 1 in VX_PAIRS else nc.scalar.copy)
-        index = 4
-        for s in range(index, LEAD):
-            dx_group(index)
-            index = index + 1
+        b_quantize(0, 0, turned[0])
+        db_shift(0, 0)
+        db_shift(1, 0)
+        b_quantize(0, 1, turned[1])
+        db_shift(0, 1)
 
-        quarters = [(d, j, nh) for d in range(8) for j in range(2) for nh in range(2)]
-        banks = {}
-        turned = {}
-        waiting = []
-        stores = {}
-        ready, unit, since, budget = 2, 4, SINCE, 0
-        for n in range(-DB_LEAD, 32):
+        x_interleave(0, 0, nc.scalar.copy)
+        turned = [b_turn(1, 0)]
+        dx_bank(0)
+        dx_bank(1)
+        x_interleave(0, 1, nc.vector.tensor_copy)
+        turned.append(b_turn(1, 1))
+        b_quantize(1, 0, turned[0])
+        db_shift(1, 1)
+        dx_bank(2)
+        dx_bank(3)
+        lift(2)
+        b_quantize(1, 1, turned[1])
+        x_quantize(0)
+        x_interleave(1, 0, nc.scalar.copy)
+        x_interleave(1, 1, nc.vector.tensor_copy)
+        for index in range(PACK, DX_BEFORE):
+            dx_bank(index)
+
+        db_order = [(d, j, nh) for d in range(PAIRS) for j in range(2) for nh in range(2)]
+        to_turn = [(kc, nh) for kc in range(2, 4) for nh in range(2)]
+        db_banks, late_turned, dx_stores = {}, {}, {}
+        dx_next = DX_BEFORE
+        for n in range(-DB_LEAD, DB_BANKS):
             d, q = divmod(n, 4)
-            if n - TURN_LAG in turned:
-                waiting.extend(turned[n - TURN_LAG])
             if n >= 0 and q == 2:
-                if 3 <= d + LIFT_LEAD < 8 and d + LIFT_LEAD not in SIGN_PAIRS:
+                if d + LIFT_LEAD < PAIRS:
                     lift(d + LIFT_LEAD)
-            if n >= 0 and q in QUANT_AT:
-                for item in waiting:
-                    b_quant(*item)
-                    ready = ready + 1
-                waiting = []
-            if n >= 0 and q == 2 and d + 1 < 8:
-                x_quant(d + 1)
-                if d + 2 in VX_PAIRS:
-                    x_inter(d + 2, 1, nc.vector.tensor_copy)
-                if d + 2 < 8:
-                    for grp in range(POOL_GROUPS):
-                        x_inter(d + 2, grp)
-            if q % 2 == 0 and 4 <= n // 2 + SHIFT_LEAD < 16:
+                if (d + 1, 1) in late_turned:
+                    for nh in range(2):
+                        b_quantize(d + 1, nh, late_turned[d + 1, nh])
+                if d + 1 < PAIRS:
+                    x_quantize(d + 1)
+                if d + 2 < PAIRS and d % 2 == 1:
+                    x_interleave(d + 2, 1, nc.vector.tensor_copy)
+            if q % 2 == 0 and 2 * POOL_FROM <= n // 2 + SHIFT_LEAD < 2 * PAIRS:
                 db_shift(*divmod(n // 2 + SHIFT_LEAD, 2))
-            if n + DB_LEAD < 32:
-                banks[n + DB_LEAD] = db_product(*quarters[n + DB_LEAD])
-            budget = budget + FILL_NUM
-            while budget >= FILL_DEN:
-                unlocked = index < (FIRST[0], 16, 16 + FIRST[1], 32)[min(3, ready // 2)]
-                if unit < 8 and (since >= DX_PER_TURN or not unlocked):
-                    turned.setdefault(n, []).append((unit // 2, unit % 2, b_turn(unit // 2, unit % 2)))
-                    unit, since, budget = unit + 1, 0, budget - 2 * FILL_DEN
-                elif unlocked and index < 32:
-                    dx_group(index)
-                    index, since, budget = index + 1, since + 1, budget - FILL_DEN
-                else:
-                    budget = 0
-            xd, xq = divmod(n + XS_LEAD, 4)
-            if 2 <= xd < 8 and xq in XS_AT[POOL_GROUPS:] and not (xd in VX_PAIRS and xq == XS_AT[1]):
-                x_inter(xd, XS_AT.index(xq))
-            stores[n + STORE_LAG] = list(dx_done)
-            dx_done.clear()
-            for dst, src in stores.get(n, []):
+            if n + DB_LEAD < DB_BANKS:
+                db_banks[n + DB_LEAD] = db_product(*db_order[n + DB_LEAD])
+            if n % 2 == 1 and to_turn:
+                late_turned[to_turn[0]] = b_turn(*to_turn[0])
+                to_turn = to_turn[1:]
+            else:
+                for index in range(dx_next, min(dx_next + 1 + n % 2, DX_BANKS)):
+                    dx_bank(index)
+                    dx_next = index + 1
+            xd, xq = divmod(n + INTERLEAVE_LEAD, 4)
+            if 2 <= xd < PAIRS and (xq == 0 or (xq == 2 and xd % 2 == 0)):
+                x_interleave(xd, xq // 2, nc.scalar.copy)
+            dx_stores[n + DB_LEAD] = list(dx_ready)
+            dx_ready.clear()
+            for dst, src in dx_stores.get(n, []):
                 nc.sync.dma_start(out=dst, in_=src)
-            if (n + SIGN_LEAD) // 4 in SIGN_PAIRS:
-                sign(*divmod(n + SIGN_LEAD, 4))
             if n >= 0:
-                db_add(*quarters[n], banks[n])
-        assert index == 32 and not any(stores[n] for n in stores if n >= 32)
+                db_add(*db_order[n], db_banks[n])

@@ -38,7 +38,7 @@ DB_LEAD = BANKS["vector"] - 1
 SHIFT_LEAD = 4
 LIFT_LEAD = SHIFT_LEAD // 2 + 1
 INTERLEAVE_LEAD = 9
-DX_BEFORE = 6
+DX_BEFORE = 7
 POOL_FROM = 2
 
 
@@ -207,18 +207,24 @@ def tile_advresnet_v_kernel(
                     )
 
         def keep_diagonal(nh, bank):
-            nc.vector.scalar_tensor_tensor(
-                out=diag[:, half(nh)].rearrange("p (q c) -> p q c", q=4),
-                in0=bank[:].rearrange("p (q c) -> p q c", q=4),
-                scalar=-EPSILON,
-                in1=ident[:].unsqueeze(1).to_broadcast([P, 4, P]),
-                op0=ALU.mult,
-                op1=ALU.mult,
-            )
+            for q in range(4):
+                block = 4 * nh + q
+                nc.vector.scalar_tensor_tensor(
+                    out=masked[:, block * P : (block + 1) * P],
+                    in0=bank[:, q * P : (q + 1) * P],
+                    scalar=-EPSILON,
+                    in1=inv_step[:],
+                    op0=ALU.mult,
+                    op1=ALU.mult,
+                    accum_out=shift_col[:, block : block + 1],
+                )
 
         def spread_shift(nh):
             bank = new_bank("shift%d" % nh, "shift" if nh == 0 else "scalar")
-            nc.tensor.matmul(out=bank[:], lhsT=inv_step[:], rhs=diag[:, half(nh)], start=True, stop=True)
+            for q in range(4):
+                block = 4 * nh + q
+                column = shift_col[:, block : block + 1].to_broadcast([P, P])
+                nc.tensor.transpose(bank[:, q * P : (q + 1) * P], column, ident[:])
             shift[nh] = bank
             if nh == 1:
                 shift[nh] = keep.tile([P, BANK], F32, name="shift_high")
@@ -269,7 +275,8 @@ def tile_advresnet_v_kernel(
 
         ident = keep.tile([P, P], F32, name="ident")
         inv_step = keep.tile([P, P], F32, name="inv_step")
-        diag = keep.tile([P, N], F32, name="diag")
+        shift_col = keep.tile([P, N // P], F32, name="shift_col")
+        masked = keep.tile([P, N], F32, name="masked")
 
         for grp in range(2):
             load_tokens(g_raw, "g", grad_out, grp)
@@ -279,21 +286,18 @@ def tile_advresnet_v_kernel(
             load_beta(2 * kh + 1)
             load_x(kh)
         make_identity(nc, ident[:])
-        nc.vector.memset(inv_step[:], 1.0 / STEP)
+        nc.vector.tensor_single_scalar(out=inv_step[:], in_=ident[:], scalar=1.0 / STEP, op=ALU.mult)
 
         gy = [new_bank("gy%d" % nh, "vector") for nh in range(2)]
         mixed = [g_interleave(0, nh) for nh in range(2)]
         turned = [g_turn(0, nh) for nh in range(2)]
         for nh in range(2):
             g_tok_quantize(0, nh, mixed[nh])
-        gy_blocks(gy[0], 0, 0, range(4))
         for nh in range(2):
+            gy_blocks(gy[nh], nh, 0, range(4))
             g_feat_quantize(0, nh, turned[nh])
         mixed = [g_interleave(1, nh) for nh in range(2)]
-        turned = []
-        for nh in range(2):
-            gy_blocks(gy[1], 1, 0, range(2 * nh, 2 * nh + 2))
-            turned.append(g_turn(1, nh))
+        turned = [g_turn(1, nh) for nh in range(2)]
         for nh in range(2):
             gy_blocks(gy[nh], nh, 1, range(4))
         g_feat_quantize(1, 0, turned[0])
@@ -307,29 +311,25 @@ def tile_advresnet_v_kernel(
         for nh in range(2):
             turned.append(b_turn(0, nh))
             spread_shift(nh)
-        lift(0)
-        lift(1)
-        b_quantize(0, 0, turned[0])
-        db_shift(0, 0)
-        db_shift(1, 0)
-        b_quantize(0, 1, turned[1])
-        db_shift(0, 1)
-
+        for nh in range(2):
+            turned.append(b_turn(1, nh))
+        for nh in range(2):
+            b_quantize(0, nh, turned[nh])
+            lift(nh)
         x_interleave(0, 0, nc.scalar.copy)
-        turned = [b_turn(1, 0)]
-        dx_bank(0)
-        dx_bank(1)
+        for nh in range(2):
+            db_shift(0, nh)
+            b_quantize(1, nh, turned[2 + nh])
+
+        for index in range(PACK):
+            dx_bank(index)
         x_interleave(0, 1, nc.vector.tensor_copy)
-        turned.append(b_turn(1, 1))
-        b_quantize(1, 0, turned[0])
-        db_shift(1, 1)
-        dx_bank(2)
-        dx_bank(3)
-        lift(2)
-        b_quantize(1, 1, turned[1])
+        db_shift(1, 0)
         x_quantize(0)
         x_interleave(1, 0, nc.scalar.copy)
         x_interleave(1, 1, nc.vector.tensor_copy)
+        db_shift(1, 1)
+        lift(2)
         for index in range(PACK, DX_BEFORE):
             dx_bank(index)
 

from contextlib import ExitStack

import concourse.mybir as mybir
from concourse.masks import make_identity

B, K, N = 1024, 2048, 1024
EPSILON = 0.1
FLOPS = 2 * 2 * B * K * N
BYTES = 2 * (B * K + 2 * B * N + K * N) + 4 * (B * K + K * N)

F32 = mybir.dt.float32
BF16 = mybir.dt.bfloat16
U32 = mybir.dt.uint32
U8 = mybir.dt.uint8
E4M3 = mybir.dt.float8_e4m3fn_x4
E5M2 = mybir.dt.float8_e5m2_x4
ALU = mybir.AluOpType

P = 128
PACK = 4
PASS = P * PACK
BANK = 512
HALF_K = K // 2
PAIR = 2 * P
PAIRS = K // PAIR
DX_BANKS = (B // P) * (K // BANK)
DB_BANKS = (K // P) * (N // BANK)

LIFT = 2.0**100
STEP = 2.0**-33

BANKS = {"vector": 3, "scalar": 4, "shift": 1}
WIDE_BUFS = 8
TURNED_BUFS = 4
INTERLEAVED_BUFS = 4

DB_LEAD = BANKS["vector"] - 1
SHIFT_LEAD = 4
LIFT_LEAD = SHIFT_LEAD // 2 + 1
INTERLEAVE_LEAD = 9
DX_BEFORE = 7
POOL_FROM = 2


def tile_advresnet_v_kernel(
    tc, x, y, beta, bias_lin, W1, W2, bias1, bias2, adv, grad_out, out_0, out_1
):
    nc = tc.nc
    assert adv == 1
    with ExitStack() as ctx:
        keep = ctx.enter_context(tc.tile_pool(name="keep", bufs=1))
        work = ctx.enter_context(tc.tile_pool(name="work", bufs=1))
        wide = ctx.enter_context(tc.tile_pool(name="wide", bufs=WIDE_BUFS))
        psum = ctx.enter_context(tc.psum_pool(name="psum", bufs=1))
        ctx.enter_context(tc.manual_schedule())

        g_raw, y_raw, b_raw, x_raw = {}, {}, {}, {}
        g_tok = [[None, None], [None, None]]
        g_feat = [[None, None], [None, None]]
        b_feat = [[None, None] for kc in range(K // BANK)]
        x_tok, x_mixed, dx_rows, db_rows, lifted, shift = {}, {}, {}, {}, {}, {}
        dx_ready = []

        def half(nh):
            return slice(nh * BANK, (nh + 1) * BANK)

        def token_rows(src, grp, cols):
            return src[grp * PASS : (grp + 1) * PASS, cols].rearrange("(p s) w -> p s w", s=PACK)

        def load_tokens(tiles, name, src, grp):
            tiles[grp] = wide.tile([P, PACK, N], BF16, name="%s%d" % (name, grp), tag="wide", align_bytes=64)
            nc.sync.dma_start(out=tiles[grp][:], in_=token_rows(src, grp, slice(0, N)))

        def load_beta(kc):
            b_raw[kc] = keep.tile([P, PACK, N], BF16, name="b%d" % kc, align_bytes=64)
            nc.sync.dma_start(
                out=b_raw[kc][:].rearrange("p (e j) n -> p e (j n)", j=2),
                in_=beta[kc * BANK : (kc + 1) * BANK, :].rearrange("(e p j) n -> p e (j n)", p=P, j=2),
            )

        def load_x(kh):
            for grp in range(2):
                x_raw[kh, grp] = keep.tile([P, PACK, HALF_K], BF16, name="x%d%d" % (kh, grp))
                cols = slice(kh * HALF_K, (kh + 1) * HALF_K)
                nc.sync.dma_start(out=x_raw[kh, grp][:], in_=token_rows(x, grp, cols))

        def new_bank(name, reader):
            bank = psum.tile([P, BANK], F32, name=name, tag=reader, bufs=BANKS[reader])
            return bank

        def new_interleaved(name):
            mixed = work.tile([P, BANK * PACK], BF16, name=name, tag="mixed", bufs=INTERLEAVED_BUFS, align_bytes=64)
            return mixed

        def turn(name, raw, nh):
            words = raw[:].bitcast(F32)
            w0 = nh * PASS // 2
            banks = []
            for two in range(2):
                banks.append(new_bank("%s_ps%d" % (name, two), "scalar"))
                for a in range(2):
                    for u in range(2):
                        c0 = (2 * a + u) * P
                        nc.tensor.transpose(
                            banks[two][:, c0 : c0 + P], words[:, 2 * two + a, w0 + u : w0 + PASS // 2 : 2], ident[:]
                        )
            turned = work.tile([P, BANK * PACK], BF16, name=name, tag="turned", bufs=TURNED_BUFS, align_bytes=64)
            for two in range(2):
                dst = turned[:].bitcast(F32)[:, two * BANK : (two + 1) * BANK]
                nc.scalar.copy(
                    out=dst.rearrange("p (a c u) -> p a c u", a=2, u=2),
                    in_=banks[two][:].rearrange("p (a u c) -> p a c u", a=2, u=2),
                )
            return turned

        def quantize(name, values, fmt):
            codes = keep.tile([P, BANK], U32, name=name + "_codes", align_bytes=64)
            scales = keep.tile([P, BANK], U8, name=name + "_scales", align_bytes=64)
            nc.vector.quantize_mx(out=codes[:].bitcast(fmt), scales=scales[:], in_=values[:])
            return codes, scales, fmt

        def product(name, reader, stationary, moving):
            bank = new_bank(name, reader)
            for g in range(2):
                (l_codes, l_scales, l_fmt), m = stationary[g]
                cols = slice(m * P, (m + 1) * P)
                r_codes, r_scales, r_fmt = moving[g]
                nc.tensor.matmul_mx(
                    out=bank[:],
                    lhsT=l_codes[:, cols].bitcast(l_fmt),
                    lhsT_scale=l_scales[:, cols],
                    rhs=r_codes[:].bitcast(r_fmt),
                    rhs_scale=r_scales[:],
                    start=(g == 0),
                    stop=(g == 1),
                )
            return bank

        def g_interleave(grp, nh):
            mixed = new_interleaved("gi%d%d" % (grp, nh))
            nc.vector.tensor_copy(
                out=mixed[:].rearrange("p (c i s) -> p c s i", i=4, s=PACK),
                in_=g_raw[grp][:, :, half(nh)].rearrange("p s (c i) -> p c s i", i=4),
            )
            return mixed

        def g_tok_quantize(grp, nh, mixed):
            g_tok[nh][grp] = quantize("gtok%d%d" % (nh, grp), mixed, E5M2)

        def g_turn(grp, nh):
            return turn("gt%d%d" % (grp, nh), g_raw[grp], nh)

        def g_feat_quantize(grp, nh, turned):
            g_feat[grp][nh] = quantize("gfeat%d%d" % (grp, nh), turned, E5M2)

        def b_turn(kc, nh):
            return turn("bt%d%d" % (kc, nh), b_raw[kc], nh)

        def b_quantize(kc, nh, turned):
            b_feat[kc][nh] = quantize("bfeat%d%d" % (kc, nh), turned, E4M3)

        def x_interleave(d, grp, copy):
            if grp == 0:
                x_mixed[d] = new_interleaved("xi%d" % d)
            kh, c0 = divmod(d * PAIR, HALF_K)
            dst = x_mixed[d][:, grp * PAIR * PACK : (grp + 1) * PAIR * PACK]
            copy(
                out=dst.rearrange("p (j c m s) -> p c s m j", j=2, m=2, s=PACK),
                in_=x_raw[kh, grp][:, :, c0 : c0 + PAIR].rearrange("p s (c m j) -> p c s m j", m=2, j=2),
            )

        def x_quantize(d):
            x_tok[d] = quantize("xtok%d" % d, x_mixed[d], E4M3)

        dx_order = [(0, s, kc) for kc in range(2) for s in range(PACK)]
        dx_order = dx_order + [(1, s, kc) for s in range(PACK) for kc in range(2)]
        dx_order = dx_order + [(grp, s, kc) for grp in range(2) for s in range(PACK) for kc in range(2, 4)]

        def dx_bank(index):
            grp, s, kc = dx_order[index]
            kh, side = divmod(kc, 2)
            two, a = divmod(s, 2)
            if side == 0 and a == 0:
                name = "dx%d%d%d" % (grp, two, kh)
                dx_rows[grp, two] = wide.tile([P, 2, HALF_K], F32, name=name, tag="wide", align_bytes=64)
            rows = dx_rows[grp, two]
            stationary = [(g_feat[grp][nh], s) for nh in range(2)]
            bank = product("dx_ps%d%d%d" % (grp, s, kc), "scalar", stationary, b_feat[kc])
            nc.scalar.copy(
                out=rows[:, a, half(side)].rearrange("p (e c j) -> p e c j", e=2, j=2),
                in_=bank[:].rearrange("p (e j c) -> p e c j", e=2, j=2),
            )
            if side == 1:
                dst = token_rows(out_0, grp, slice(kh * HALF_K, (kh + 1) * HALF_K))
                dx_ready.append((dst[:, s, :], rows[:, a, :]))

        def gy_blocks(bank, nh, grp, blocks):
            for q in blocks:
                cols = slice(nh * BANK + q * P, nh * BANK + (q + 1) * P)
                for s in range(PACK):
                    nc.tensor.matmul(
                        out=bank[:, q * P : (q + 1) * P],
                        lhsT=g_raw[grp][:, s, cols],
                        rhs=y_raw[grp][:, s, cols],
                        start=(grp == 0 and q == 0 and s == 0),
                        stop=(grp == 1 and q == 3 and s == PACK - 1),
                    )

        def keep_diagonal(nh, bank):
            for q in range(4):
                block = 4 * nh + q
                nc.vector.scalar_tensor_tensor(
                    out=masked[:, block * P : (block + 1) * P],
                    in0=bank[:, q * P : (q + 1) * P],
                    scalar=-EPSILON,
                    in1=inv_step[:],
                    op0=ALU.mult,
                    op1=ALU.mult,
                    accum_out=shift_col[:, block : block + 1],
                )

        def spread_shift(nh):
            bank = new_bank("shift%d" % nh, "shift" if nh == 0 else "scalar")
            for q in range(4):
                block = 4 * nh + q
                column = shift_col[:, block : block + 1].to_broadcast([P, P])
                nc.tensor.transpose(bank[:, q * P : (q + 1) * P], column, ident[:])
            shift[nh] = bank
            if nh == 1:
                shift[nh] = keep.tile([P, BANK], F32, name="shift_high")
                nc.scalar.copy(out=shift[nh][:], in_=bank[:])

        def lift(d):
            kc, e = divmod(d, 2)
            lifted[d] = work.tile([P, 2, N], BF16, name="lifted%d" % d, tag="lifted", bufs=2)
            nc.vector.tensor_scalar(
                out=lifted[d][:].rearrange("p j n -> p (j n)"),
                in0=b_raw[kc][:, 2 * e : 2 * e + 2, :].rearrange("p j n -> p (j n)"),
                scalar1=LIFT,
                scalar2=-STEP,
                op0=ALU.mult,
                op1=ALU.max,
            )

        def db_shift(d, nh):
            if nh == 0:
                db_rows[d] = wide.tile([P, 2, N], F32, name="db%d" % d, tag="wide", align_bytes=64)
            row = shift[nh][:].unsqueeze(1).to_broadcast([P, 2, BANK])
            if nh == 1 and d >= POOL_FROM:
                signs = work.tile([P, 2, BANK], BF16, name="signs%d" % d, tag="signs", bufs=1)
                nc.vector.tensor_single_scalar(out=signs[:], in_=lifted[d][:, :, half(nh)], scalar=STEP, op=ALU.min)
                nc.gpsimd.tensor_tensor(out=db_rows[d][:, :, half(nh)], in0=signs[:], in1=row, op=ALU.mult)
            else:
                nc.vector.scalar_tensor_tensor(
                    out=db_rows[d][:, :, half(nh)],
                    in0=lifted[d][:, :, half(nh)],
                    scalar=STEP,
                    in1=row,
                    op0=ALU.min,
                    op1=ALU.mult,
                )

        def db_product(d, j, nh):
            stationary = [(x_tok[d], 2 * grp + j) for grp in range(2)]
            return product("db_ps%d%d%d" % (d, j, nh), "vector", stationary, g_tok[nh])

        def db_add(d, j, nh, bank):
            rows = db_rows[d]
            nc.vector.tensor_tensor(out=rows[:, j, half(nh)], in0=bank[:], in1=rows[:, j, half(nh)], op=ALU.add)
            dst = out_1[d * PAIR : (d + 1) * PAIR, :].rearrange("(p j) n -> p j n", j=2)
            if d == PAIRS - 1 and j == 1:
                nc.sync.dma_start(out=dst[:, j, half(nh)], in_=rows[:, j, half(nh)])
            elif nh == 1:
                nc.sync.dma_start(out=dst[:, j, :], in_=rows[:, j, :])

        ident = keep.tile([P, P], F32, name="ident")
        inv_step = keep.tile([P, P], F32, name="inv_step")
        shift_col = keep.tile([P, N // P], F32, name="shift_col")
        masked = keep.tile([P, N], F32, name="masked")

        for grp in range(2):
            load_tokens(g_raw, "g", grad_out, grp)
            load_tokens(y_raw, "y", y, grp)
        for kh in range(2):
            load_beta(2 * kh)
            load_beta(2 * kh + 1)
            load_x(kh)
        make_identity(nc, ident[:])
        nc.vector.tensor_single_scalar(out=inv_step[:], in_=ident[:], scalar=1.0 / STEP, op=ALU.mult)

        gy = [new_bank("gy%d" % nh, "vector") for nh in range(2)]
        mixed = [g_interleave(0, nh) for nh in range(2)]
        turned = [g_turn(0, nh) for nh in range(2)]
        for nh in range(2):
            g_tok_quantize(0, nh, mixed[nh])
        for nh in range(2):
            gy_blocks(gy[nh], nh, 0, range(4))
            g_feat_quantize(0, nh, turned[nh])
        mixed = [g_interleave(1, nh) for nh in range(2)]
        turned = [g_turn(1, nh) for nh in range(2)]
        for nh in range(2):
            gy_blocks(gy[nh], nh, 1, range(4))
        g_feat_quantize(1, 0, turned[0])
        for nh in range(2):
            g_tok_quantize(1, nh, mixed[nh])
        keep_diagonal(0, gy[0])
        g_feat_quantize(1, 1, turned[1])
        keep_diagonal(1, gy[1])

        turned = []
        for nh in range(2):
            turned.append(b_turn(0, nh))
            spread_shift(nh)
        for nh in range(2):
            turned.append(b_turn(1, nh))
        for nh in range(2):
            b_quantize(0, nh, turned[nh])
            lift(nh)
        x_interleave(0, 0, nc.scalar.copy)
        for nh in range(2):
            db_shift(0, nh)
            b_quantize(1, nh, turned[2 + nh])

        for index in range(PACK):
            dx_bank(index)
        x_interleave(0, 1, nc.vector.tensor_copy)
        db_shift(1, 0)
        x_quantize(0)
        x_interleave(1, 0, nc.scalar.copy)
        x_interleave(1, 1, nc.vector.tensor_copy)
        db_shift(1, 1)
        lift(2)
        for index in range(PACK, DX_BEFORE):
            dx_bank(index)

        db_order = [(d, j, nh) for d in range(PAIRS) for j in range(2) for nh in range(2)]
        to_turn = [(kc, nh) for kc in range(2, 4) for nh in range(2)]
        db_banks, late_turned, dx_stores = {}, {}, {}
        dx_next = DX_BEFORE
        for n in range(-DB_LEAD, DB_BANKS):
            d, q = divmod(n, 4)
            if n >= 0 and q == 2:
                if d + LIFT_LEAD < PAIRS:
                    lift(d + LIFT_LEAD)
                if (d + 1, 1) in late_turned:
                    for nh in range(2):
                        b_quantize(d + 1, nh, late_turned[d + 1, nh])
                if d + 1 < PAIRS:
                    x_quantize(d + 1)
                if d + 2 < PAIRS and d % 2 == 1:
                    x_interleave(d + 2, 1, nc.vector.tensor_copy)
            if q % 2 == 0 and 2 * POOL_FROM <= n // 2 + SHIFT_LEAD < 2 * PAIRS:
                db_shift(*divmod(n // 2 + SHIFT_LEAD, 2))
            if n + DB_LEAD < DB_BANKS:
                db_banks[n + DB_LEAD] = db_product(*db_order[n + DB_LEAD])
            if n % 2 == 1 and to_turn:
                late_turned[to_turn[0]] = b_turn(*to_turn[0])
                to_turn = to_turn[1:]
            else:
                for index in range(dx_next, min(dx_next + 1 + n % 2, DX_BANKS)):
                    dx_bank(index)
                    dx_next = index + 1
            xd, xq = divmod(n + INTERLEAVE_LEAD, 4)
            if 2 <= xd < PAIRS and (xq == 0 or (xq == 2 and xd % 2 == 0)):
                x_interleave(xd, xq // 2, nc.scalar.copy)
            dx_stores[n + DB_LEAD] = list(dx_ready)
            dx_ready.clear()
            for dst, src in dx_stores.get(n, []):
                nc.sync.dma_start(out=dst, in_=src)
            if n >= 0:
                db_add(*db_order[n], db_banks[n])
